import numpy as np
import ml_dtypes


def mxq(x, axis, fmt="e4m3"):
    dtype, down = {"e4m3": (ml_dtypes.float8_e4m3fn, 7), "e5m2": (ml_dtypes.float8_e5m2, 14)}[fmt]
    v = np.moveaxis(np.asarray(x, np.float32).astype(ml_dtypes.bfloat16).astype(np.float64), axis, -1)
    blocks = v.reshape(v.shape[:-1] + (-1, 32))
    amax = np.abs(blocks).max(-1, keepdims=True)
    byte = np.maximum(np.where(amax > 0, np.frexp(amax)[1] - 1 + 127, 0) - down, 1)
    scale = np.exp2(byte - 127.0)
    codes = (blocks / scale).astype(np.float32).astype(dtype).astype(np.float64)
    return np.moveaxis((codes * scale).reshape(v.shape), -1, axis)


WIDE = False


def mx_kscale(k):
    if not WIDE:
        return np.ones(k)
    levels = np.array([10, -10, 5, -5, 0])
    a = np.random.permutation(np.resize(levels, k // 512 * 4)).reshape(k // 512, 4)
    idx = np.arange(k)
    return np.exp2(a[idx // 512, idx % 128 // 32])


BF16 = ml_dtypes.bfloat16


def bf(x):
    return np.asarray(x, np.float32).astype(BF16)


def f64(x):
    return np.asarray(x).astype(np.float64)


B, S, IN_DIM, OUT_DIM, R = 4, 1024, 512, 1280, 512
RB1 = -(-OUT_DIM // R)
PAD = R * RB1 - OUT_DIM
HALF = R // 2
ROPE_BASE = 10000.0


def freqs():
    inv_freq = 1.0 / ROPE_BASE ** (np.arange(0, R, 2) / R)
    emb = np.outer(np.arange(RB1) * 1.0, inv_freq)
    emb = np.concatenate([emb, emb], axis=-1)
    return np.cos(emb), np.sin(emb)


def setup_inputs():
    s = mx_kscale(IN_DIM)
    return {"x": bf(np.random.standard_normal((B, S, IN_DIM)) * s),
            "weight": bf(np.random.standard_normal((OUT_DIM, IN_DIM)) / np.sqrt(IN_DIM) / s),
            "lora_a_weight": bf(np.random.standard_normal((R, R)) * 0.5 / np.sqrt(R))}


def reference(x, weight, lora_a_weight):
    h = mxq(f64(x), 2, "e4m3") @ mxq(f64(weight), 1, "e4m3").T
    cos, sin = freqs()
    z = np.concatenate([h, h[..., :PAD]], axis=-1)
    z = z.reshape(*z.shape[:-1], RB1, R)
    rh = np.concatenate([-z[..., HALF:], z[..., :HALF]], axis=-1)
    z = z * cos + rh * sin
    y = mxq(z, 3, "e4m3") @ mxq(f64(lora_a_weight), 1, "e4m3").T
    y = y.reshape(*y.shape[:-2], RB1 * R)[..., :OUT_DIM]
    return h + y

@@ -1,0 +1,277 @@
+import math
+from contextlib import ExitStack
+
+import concourse.bass as bass
+import concourse.mybir as mybir
+import concourse.tile as tile
+from concourse.masks import make_identity
+
+F32 = mybir.dt.float32
+BF16 = mybir.dt.bfloat16
+U32 = mybir.dt.uint32
+U8 = mybir.dt.uint8
+I32 = mybir.dt.int32
+FP8X4 = mybir.dt.float8_e4m3fn_x4
+ACT = mybir.ActivationFunctionType
+ALU = mybir.AluOpType
+
+P = 128
+TOKENS = 4096
+IN_DIM = 512
+OUT_DIM = 1280
+R = 512
+HB = 256
+N_HB = TOKENS // HB
+W_TILES = OUT_DIM // P
+SLOT_TO_CHUNK = (0, 2, 1, 3)
+PIN = False
+
+FLOPS = 2 * TOKENS * IN_DIM * OUT_DIM + 2 * TOKENS * R * 3 * R
+
+
+def tile_moralinear_pa_t_kernel(tc, x, weight, lora_a_weight, out):
+    nc = tc.nc
+    x_blocks = x.flatten_outer_dims().rearrange("(b p i) k -> b p (i k)", p=P, i=4)
+    out_blocks = out.flatten_outer_dims().rearrange("(b p i) c -> b p (i c)", p=P, i=4)
+    w_pairs = weight.rearrange("(q j p) k -> q p j k", j=2, p=P)
+    a_rows = lora_a_weight.rearrange("(j p) r -> p j r", p=P)
+
+    with ExitStack() as ctx:
+        const = ctx.enter_context(tc.tile_pool(name="const", bufs=1))
+        xin = ctx.enter_context(tc.tile_pool(name="xin", bufs=8))
+        win = ctx.enter_context(tc.tile_pool(name="win", bufs=5))
+        grp = ctx.enter_context(tc.tile_pool(name="grp", bufs=3))
+        xq = ctx.enter_context(tc.tile_pool(name="xq", bufs=4))
+        vpool = ctx.enter_context(tc.tile_pool(name="vpool", bufs=4))
+        gpool = ctx.enter_context(tc.tile_pool(name="gpool", bufs=3))
+        zq = ctx.enter_context(tc.tile_pool(name="zq", bufs=3))
+        opool = ctx.enter_context(tc.tile_pool(name="opool", bufs=3))
+        psum_x = ctx.enter_context(tc.psum_pool(name="psum_x", bufs=1))
+        psum_s = ctx.enter_context(tc.psum_pool(name="psum_s", bufs=4))
+        psum_o = ctx.enter_context(tc.psum_pool(name="psum_o", bufs=3))
+        if PIN:
+            ctx.enter_context(tc.manual_schedule())
+
+        x_raw = []
+        w_raw = []
+        xr0 = xin.tile([P, 4 * IN_DIM], BF16, name="x_raw", tag="x_raw")
+        nc.sync.dma_start(out=xr0[:], in_=x_blocks[0])
+        x_raw.append(xr0)
+        for q in range(W_TILES // 2):
+            wr = win.tile([P, 2, IN_DIM], BF16, name="w_raw", tag="w_raw")
+            nc.sync.dma_start(out=wr[:], in_=w_pairs[q])
+            w_raw.append(wr)
+        a_raw = const.tile([P, 4, R], BF16)
+        nc.sync.dma_start(out=a_raw[:], in_=a_rows)
+        for b in range(1, TOKENS // 512):
+            xr = xin.tile([P, 4 * IN_DIM], BF16, name="x_raw", tag="x_raw")
+            nc.sync.dma_start(out=xr[:], in_=x_blocks[b])
+            x_raw.append(xr)
+
+        j_int = const.tile([P, 2], I32)
+        nc.gpsimd.iota(j_int[:], pattern=[[P, 2]], base=0, channel_multiplier=1)
+        ident_f = const.tile([P, P], F32)
+        make_identity(nc, ident_f[:])
+        ident_b = const.tile([P, P], BF16)
+        make_identity(nc, ident_b[:])
+
+        j_f = const.tile([P, 2], F32)
+        nc.vector.tensor_copy(out=j_f[:], in_=j_int[:])
+        theta = const.tile([P, 2], F32)
+        nc.scalar.activation(out=theta[:], in_=j_f[:], func=ACT.Exp, scale=-math.log(10000.0) / 256.0)
+        ang = const.tile([P, 4], F32)
+        nc.vector.tensor_copy(out=ang[:, 0:2], in_=theta[:])
+        nc.vector.tensor_scalar(out=ang[:, 2:4], in0=theta[:], scalar1=2.0, scalar2=None, op0=ALU.mult)
+        sin_t = const.tile([P, 4], F32)
+        nc.scalar.activation(out=sin_t[:], in_=ang[:], func=ACT.Sin)
+        half_t = const.tile([P, 4], F32)
+        nc.scalar.activation(out=half_t[:], in_=ang[:], func=ACT.Sin, scale=0.5)
+        nsin_t = const.tile([P, 4], F32)
+        nc.vector.tensor_scalar(out=nsin_t[:], in0=sin_t[:], scalar1=-1.0, scalar2=None, op0=ALU.mult)
+        sq_t = const.tile([P, 4], F32)
+        nc.vector.tensor_tensor(out=sq_t[:], in0=half_t[:], in1=half_t[:], op=ALU.mult)
+        cos_t = const.tile([P, 4], F32)
+        nc.vector.tensor_scalar(out=cos_t[:], in0=sq_t[:], scalar1=-2.0, scalar2=1.0, op0=ALU.mult, op1=ALU.add)
+
+        w_codes = const.tile([P, OUT_DIM], U32, align_bytes=64)
+        w_scales = const.tile([P, OUT_DIM], U8, align_bytes=64)
+        a_codes = const.tile([P, R], U32, align_bytes=64)
+        a_scales = const.tile([P, R], U8, align_bytes=64)
+        a_grp = const.tile([P, R, 4], BF16, align_bytes=64)
+
+        state = {}
+
+        def word_transposes(bank, raw_words, first):
+            for i in range(2):
+                for u in range(2):
+                    c0 = first + 256 * i + 128 * u
+                    nc.tensor.transpose(bank[:, i, u, :], raw_words[:, c0 : c0 + P], ident_f[:])
+
+        def words_out(engine_copy, dst, bank):
+            engine_copy(
+                out=dst[:].bitcast(F32).rearrange("p (i t u) -> p i t u", i=2, u=2),
+                in_=bank[:].rearrange("p i u t -> p i t u"),
+            )
+
+        def x_transpose(hb):
+            bank = psum_x.tile([P, 2, 2, P], F32, name="xt", tag="xt")
+            word_transposes(bank, x_raw[hb // 2][:].bitcast(F32), 512 * (hb % 2))
+            xg = grp.tile([P, 4 * HB], BF16, name="xg", tag="xg", align_bytes=64)
+            words_out(nc.scalar.copy, xg, bank)
+            state[("xg", hb)] = xg
+
+        def x_quantise(hb):
+            xc = xq.tile([P, HB], U32, name="xc", tag="xc", align_bytes=64)
+            xs = xq.tile([P, HB], U8, name="xs", tag="xs", align_bytes=64)
+            nc.vector.quantize_mx(out=xc[:].bitcast(FP8X4), scales=xs[:], in_=state[("xg", hb)][:])
+            state[("x", hb)] = (xc, xs)
+
+        def mx(out_ap, l_codes, l_scales, r_codes, r_scales, start, stop):
+            nc.tensor.matmul_mx(
+                out=out_ap,
+                lhsT=l_codes.bitcast(FP8X4),
+                lhsT_scale=l_scales,
+                rhs=r_codes.bitcast(FP8X4),
+                rhs_scale=r_scales,
+                start=start,
+                stop=stop,
+            )
+
+        def new_half(hb):
+            state[("g", hb)] = gpool.tile([P, 3, HB, 4], BF16, name="zg", tag="zg", align_bytes=64)
+            state[("zc", hb)] = zq.tile([P, 3, HB], U32, name="zc", tag="zc", align_bytes=64)
+            state[("zs", hb)] = zq.tile([P, 3, HB], U8, name="zs", tag="zs", align_bytes=64)
+
+        def plain_group(hb, i):
+            xc, xs = state[("x", hb)]
+            bank = psum_s.tile([P, 4, P], F32, name="g0", tag="s1")
+            t = slice(P * i, P * i + P)
+            for s in range(4):
+                w = slice(P * SLOT_TO_CHUNK[s], P * SLOT_TO_CHUNK[s] + P)
+                mx(bank[:, s, :], w_codes[:, w], w_scales[:, w], xc[:, t], xs[:, t], True, True)
+            nc.vector.tensor_copy(out=state[("g", hb)][:, 0, t, :], in_=bank[:].rearrange("p s t -> p t s"))
+
+        def rotated_pair(hb, n, tm):
+            xc, xs = state[("x", hb)]
+            bank = psum_s.tile([P, 2, HB], F32, name="z", tag="s1")
+            for ab in range(2):
+                jw = (4 * n + tm + 2 * ab) % W_TILES
+                w = slice(P * jw, P * jw + P)
+                mx(bank[:, ab, :], w_codes[:, w], w_scales[:, w], xc[:], xs[:], True, True)
+            k = 2 * (n - 1) + tm
+            v = vpool.tile([P, 2, HB], F32, name="v", tag="v")
+            nc.scalar.activation(out=v[:, 0, :], in_=bank[:, 1, :], func=ACT.Copy, scale=nsin_t[:, k : k + 1])
+            nc.scalar.activation(out=v[:, 1, :], in_=bank[:, 0, :], func=ACT.Copy, scale=sin_t[:, k : k + 1])
+            nc.vector.scalar_tensor_tensor(
+                out=state[("g", hb)][:, n, :, 2 * tm : 2 * tm + 2],
+                in0=bank[:].rearrange("p a t -> p t a"),
+                scalar=cos_t[:, k : k + 1],
+                in1=v[:].rearrange("p a t -> p t a"),
+                op0=ALU.mult,
+                op1=ALU.add,
+            )
+
+        def z_quantise(hb, n):
+            nc.vector.quantize_mx(
+                out=state[("zc", hb)][:, n, :].bitcast(FP8X4),
+                scales=state[("zs", hb)][:, n, :],
+                in_=state[("g", hb)][:, n, :, :].rearrange("p t s -> p (t s)"),
+            )
+
+        def out_wide(hb, i, c, copy):
+            xc, xs = state[("x", hb)]
+            zc = state[("zc", hb)]
+            zs = state[("zs", hb)]
+            t = slice(P * i, P * i + P)
+            cols = slice(512 * c, 512 * c + 512)
+            bank = psum_o.tile([P, 512], F32, name="o", tag="o")
+            mx(bank[:], xc[:, t], xs[:, t], w_codes[:, cols], w_scales[:, cols], True, False)
+            mx(bank[:], zc[:, c, t], zs[:, c, t], a_codes[:], a_scales[:], False, True)
+            copy(out=state[("o", hb)][:, i, cols], in_=bank[:])
+
+        def out_narrow(hb, copy):
+            xc, xs = state[("x", hb)]
+            zc = state[("zc", hb)]
+            zs = state[("zs", hb)]
+            bank = psum_o.tile([P, 2, 256], F32, name="o2", tag="o")
+            for i in range(2):
+                t = slice(P * i, P * i + P)
+                mx(bank[:, i, :], xc[:, t], xs[:, t], w_codes[:, 1024:1280], w_scales[:, 1024:1280], True, False)
+                mx(bank[:, i, :], zc[:, 2, t], zs[:, 2, t], a_codes[:, 0:256], a_scales[:, 0:256], False, True)
+            copy(out=state[("o", hb)][:, :, 1024:1280], in_=bank[:])
+
+        def store(hb):
+            h = hb % 2
+            nc.sync.dma_start(
+                out=out_blocks[hb // 2][:, 2 * OUT_DIM * h : 2 * OUT_DIM * (h + 1)],
+                in_=state[("o", hb)][:].rearrange("p i c -> p (i c)"),
+            )
+
+        x_transpose(0)
+        w_grp = []
+        for q in range(W_TILES // 2):
+            bank = psum_s.tile([P, 2, 2, P], F32, name="wt", tag="s1")
+            word_transposes(bank, w_raw[q][:].rearrange("p j k -> p (j k)").bitcast(F32), 0)
+            wg = grp.tile([P, 4 * 256], BF16, name="wg", tag="wg", align_bytes=64)
+            words_out(nc.vector.tensor_copy if q % 2 == 0 else nc.scalar.copy, wg, bank)
+            w_grp.append(wg)
+            if q == 0:
+                x_quantise(0)
+            if q >= 1:
+                cols = slice(256 * (q - 1), 256 * q)
+                nc.vector.quantize_mx(out=w_codes[:, cols].bitcast(FP8X4), scales=w_scales[:, cols], in_=w_grp[q - 1][:])
+        nc.vector.quantize_mx(out=w_codes[:, 1024:1280].bitcast(FP8X4), scales=w_scales[:, 1024:1280], in_=w_grp[4][:])
+
+        def a_prepare():
+            for jj in range(2):
+                bank = psum_s.tile([P, 2, 4, P], BF16, name="at", tag="s1")
+                for j in range(2):
+                    for s in range(4):
+                        r0 = P * SLOT_TO_CHUNK[s]
+                        nc.tensor.transpose(bank[:, j, s, :], a_raw[:, 2 * jj + j, r0 : r0 + P], ident_b[:])
+                nc.vector.tensor_copy(
+                    out=a_grp[:, 256 * jj : 256 * jj + 256, :].rearrange("p (j q) s -> p j q s", j=2),
+                    in_=bank[:].rearrange("p j s q -> p j q s"),
+                )
+
+        for hb in range(N_HB + 1):
+            first = hb < N_HB
+            second = hb >= 1
+            prev = hb - 1
+            tail = hb == N_HB
+            if second:
+                state[("o", prev)] = opool.tile([P, 2, OUT_DIM], F32, name="o_sb", tag="o_sb")
+            if hb + 1 < N_HB:
+                x_transpose(hb + 1)
+            if first:
+                new_half(hb)
+                plain_group(hb, 0)
+            if second:
+                z_quantise(prev, 2)
+                out_wide(prev, 0, 0, nc.scalar.copy)
+            if first:
+                plain_group(hb, 1)
+            if hb + 1 < N_HB:
+                x_quantise(hb + 1)
+            if second:
+                out_wide(prev, 1, 0, nc.vector.tensor_copy if tail else nc.scalar.copy)
+            if hb == 0:
+                a_prepare()
+            if first:
+                rotated_pair(hb, 1, 0)
+                z_quantise(hb, 0)
+            if second:
+                out_wide(prev, 0, 1, nc.scalar.copy)
+            if first:
+                rotated_pair(hb, 1, 1)
+            if hb == 0:
+                nc.vector.quantize_mx(out=a_codes[:].bitcast(FP8X4), scales=a_scales[:], in_=a_grp[:].rearrange("p q s -> p (q s)"))
+            if second:
+                out_wide(prev, 1, 1, nc.vector.tensor_copy if tail else nc.scalar.copy)
+            if first:
+                rotated_pair(hb, 2, 0)
+                z_quantise(hb, 1)
+                rotated_pair(hb, 2, 1)
+            if second:
+                out_narrow(prev, nc.scalar.copy)
+                store(prev)

@@ -24,7 +24,7 @@ HB = 256
 N_HB = TOKENS // HB
 W_TILES = OUT_DIM // P
 SLOT_TO_CHUNK = (0, 2, 1, 3)
-PIN = False
+PIN = True
 
 FLOPS = 2 * TOKENS * IN_DIM * OUT_DIM + 2 * TOKENS * R * 3 * R
 
@@ -41,9 +41,10 @@ def tile_moralinear_pa_t_kernel(tc, x, weight, lora_a_weight, out):
         xin = ctx.enter_context(tc.tile_pool(name="xin", bufs=8))
         win = ctx.enter_context(tc.tile_pool(name="win", bufs=5))
         grp = ctx.enter_context(tc.tile_pool(name="grp", bufs=3))
-        xq = ctx.enter_context(tc.tile_pool(name="xq", bufs=4))
+        xq = ctx.enter_context(tc.tile_pool(name="xq", bufs=5))
         vpool = ctx.enter_context(tc.tile_pool(name="vpool", bufs=4))
         gpool = ctx.enter_context(tc.tile_pool(name="gpool", bufs=3))
+        ppool = ctx.enter_context(tc.tile_pool(name="ppool", bufs=3))
         zq = ctx.enter_context(tc.tile_pool(name="zq", bufs=3))
         opool = ctx.enter_context(tc.tile_pool(name="opool", bufs=3))
         psum_x = ctx.enter_context(tc.psum_pool(name="psum_x", bufs=1))
@@ -101,6 +102,20 @@ def tile_moralinear_pa_t_kernel(tc, x, weight, lora_a_weight, out):
 
         state = {}
 
+        def ok(hb):
+            return 0 <= hb < N_HB
+
+        def mx(out_ap, l_codes, l_scales, r_codes, r_scales, start, stop):
+            nc.tensor.matmul_mx(
+                out=out_ap,
+                lhsT=l_codes.bitcast(FP8X4),
+                lhsT_scale=l_scales,
+                rhs=r_codes.bitcast(FP8X4),
+                rhs_scale=r_scales,
+                start=start,
+                stop=stop,
+            )
+
         def word_transposes(bank, raw_words, first):
             for i in range(2):
                 for u in range(2):
@@ -114,44 +129,58 @@ def tile_moralinear_pa_t_kernel(tc, x, weight, lora_a_weight, out):
             )
 
         def x_transpose(hb):
+            if not ok(hb):
+                return
             bank = psum_x.tile([P, 2, 2, P], F32, name="xt", tag="xt")
             word_transposes(bank, x_raw[hb // 2][:].bitcast(F32), 512 * (hb % 2))
+            state[("xt", hb)] = bank
+
+        def x_out(hb, copy):
+            if not ok(hb):
+                return
             xg = grp.tile([P, 4 * HB], BF16, name="xg", tag="xg", align_bytes=64)
-            words_out(nc.scalar.copy, xg, bank)
+            words_out(copy, xg, state[("xt", hb)])
             state[("xg", hb)] = xg
 
         def x_quantise(hb):
+            if not ok(hb):
+                return
             xc = xq.tile([P, HB], U32, name="xc", tag="xc", align_bytes=64)
             xs = xq.tile([P, HB], U8, name="xs", tag="xs", align_bytes=64)
             nc.vector.quantize_mx(out=xc[:].bitcast(FP8X4), scales=xs[:], in_=state[("xg", hb)][:])
             state[("x", hb)] = (xc, xs)
 
-        def mx(out_ap, l_codes, l_scales, r_codes, r_scales, start, stop):
-            nc.tensor.matmul_mx(
-                out=out_ap,
-                lhsT=l_codes.bitcast(FP8X4),
-                lhsT_scale=l_scales,
-                rhs=r_codes.bitcast(FP8X4),
-                rhs_scale=r_scales,
-                start=start,
-                stop=stop,
-            )
+        def new_group(hb, n):
+            state[("g", hb, n)] = gpool.tile([P, HB, 4], BF16, name="zg%d" % n, tag="zg%d" % n, align_bytes=64)
+            state[("zc", hb, n)] = zq.tile([P, HB], U32, name="zc%d" % n, tag="zc%d" % n, align_bytes=64)
+            state[("zs", hb, n)] = zq.tile([P, HB], U8, name="zs%d" % n, tag="zs%d" % n, align_bytes=64)
+            if n > 0:
+                state[("zp", hb, n)] = ppool.tile([P, 4, HB], BF16, name="zp%d" % n, tag="zp%d" % n)
 
-        def new_half(hb):
-            state[("g", hb)] = gpool.tile([P, 3, HB, 4], BF16, name="zg", tag="zg", align_bytes=64)
-            state[("zc", hb)] = zq.tile([P, 3, HB], U32, name="zc", tag="zc", align_bytes=64)
-            state[("zs", hb)] = zq.tile([P, 3, HB], U8, name="zs", tag="zs", align_bytes=64)
-
-        def plain_group(hb, i):
+        def plain_mm(hb, i):
+            if not ok(hb):
+                return
+            if i == 0:
+                new_group(hb, 0)
             xc, xs = state[("x", hb)]
             bank = psum_s.tile([P, 4, P], F32, name="g0", tag="s1")
             t = slice(P * i, P * i + P)
             for s in range(4):
                 w = slice(P * SLOT_TO_CHUNK[s], P * SLOT_TO_CHUNK[s] + P)
                 mx(bank[:, s, :], w_codes[:, w], w_scales[:, w], xc[:, t], xs[:, t], True, True)
-            nc.vector.tensor_copy(out=state[("g", hb)][:, 0, t, :], in_=bank[:].rearrange("p s t -> p t s"))
+            state[("g0", hb, i)] = bank
 
-        def rotated_pair(hb, n, tm):
+        def plain_out(hb, i):
+            if not ok(hb):
+                return
+            t = slice(P * i, P * i + P)
+            nc.vector.tensor_copy(out=state[("g", hb, 0)][:, t, :], in_=state[("g0", hb, i)][:].rearrange("p s t -> p t s"))
+
+        def rotated(hb, n, tm):
+            if not ok(hb):
+                return
+            if tm == 0:
+                new_group(hb, n)
             xc, xs = state[("x", hb)]
             bank = psum_s.tile([P, 2, HB], F32, name="z", tag="s1")
             for ab in range(2):
@@ -163,51 +192,72 @@ def tile_moralinear_pa_t_kernel(tc, x, weight, lora_a_weight, out):
             nc.scalar.activation(out=v[:, 0, :], in_=bank[:, 1, :], func=ACT.Copy, scale=nsin_t[:, k : k + 1])
             nc.scalar.activation(out=v[:, 1, :], in_=bank[:, 0, :], func=ACT.Copy, scale=sin_t[:, k : k + 1])
             nc.vector.scalar_tensor_tensor(
-                out=state[("g", hb)][:, n, :, 2 * tm : 2 * tm + 2],
-                in0=bank[:].rearrange("p a t -> p t a"),
+                out=state[("zp", hb, n)][:, 2 * tm : 2 * tm + 2, :],
+                in0=bank[:],
                 scalar=cos_t[:, k : k + 1],
-                in1=v[:].rearrange("p a t -> p t a"),
+                in1=v[:],
+                op0=ALU.mult,
+                op1=ALU.add,
+            )
+
+        def regroup(hb, n):
+            if not ok(hb):
+                return
+            nc.gpsimd.tensor_scalar(
+                out=state[("g", hb, n)][:],
+                in0=state[("zp", hb, n)][:].rearrange("p s t -> p t s"),
+                scalar1=1.0,
+                scalar2=0.0,
                 op0=ALU.mult,
                 op1=ALU.add,
             )
 
         def z_quantise(hb, n):
+            if not ok(hb):
+                return
             nc.vector.quantize_mx(
-                out=state[("zc", hb)][:, n, :].bitcast(FP8X4),
-                scales=state[("zs", hb)][:, n, :],
-                in_=state[("g", hb)][:, n, :, :].rearrange("p t s -> p (t s)"),
+                out=state[("zc", hb, n)][:].bitcast(FP8X4),
+                scales=state[("zs", hb, n)][:],
+                in_=state[("g", hb, n)][:].rearrange("p t s -> p (t s)"),
             )
 
         def out_wide(hb, i, c, copy):
+            if not ok(hb):
+                return
+            if ("o", hb) not in state:
+                state[("o", hb)] = opool.tile([P, 2, OUT_DIM], F32, name="o_sb", tag="o_sb")
             xc, xs = state[("x", hb)]
-            zc = state[("zc", hb)]
-            zs = state[("zs", hb)]
+            zc = state[("zc", hb, c)]
+            zs = state[("zs", hb, c)]
             t = slice(P * i, P * i + P)
             cols = slice(512 * c, 512 * c + 512)
             bank = psum_o.tile([P, 512], F32, name="o", tag="o")
             mx(bank[:], xc[:, t], xs[:, t], w_codes[:, cols], w_scales[:, cols], True, False)
-            mx(bank[:], zc[:, c, t], zs[:, c, t], a_codes[:], a_scales[:], False, True)
+            mx(bank[:], zc[:, t], zs[:, t], a_codes[:], a_scales[:], False, True)
             copy(out=state[("o", hb)][:, i, cols], in_=bank[:])
 
         def out_narrow(hb, copy):
+            if not ok(hb):
+                return
             xc, xs = state[("x", hb)]
-            zc = state[("zc", hb)]
-            zs = state[("zs", hb)]
+            zc = state[("zc", hb, 2)]
+            zs = state[("zs", hb, 2)]
             bank = psum_o.tile([P, 2, 256], F32, name="o2", tag="o")
             for i in range(2):
                 t = slice(P * i, P * i + P)
                 mx(bank[:, i, :], xc[:, t], xs[:, t], w_codes[:, 1024:1280], w_scales[:, 1024:1280], True, False)
-                mx(bank[:, i, :], zc[:, 2, t], zs[:, 2, t], a_codes[:, 0:256], a_scales[:, 0:256], False, True)
+                mx(bank[:, i, :], zc[:, t], zs[:, t], a_codes[:, 0:256], a_scales[:, 0:256], False, True)
             copy(out=state[("o", hb)][:, :, 1024:1280], in_=bank[:])
 
-        def store(hb):
+        def store(hb, c0, c1):
+            if not ok(hb):
+                return
+            dst = out_blocks[hb // 2].rearrange("p (i c) -> p i c", i=4)
             h = hb % 2
-            nc.sync.dma_start(
-                out=out_blocks[hb // 2][:, 2 * OUT_DIM * h : 2 * OUT_DIM * (h + 1)],
-                in_=state[("o", hb)][:].rearrange("p i c -> p (i c)"),
-            )
+            nc.sync.dma_start(out=dst[:, 2 * h : 2 * h + 2, c0:c1], in_=state[("o", hb)][:, :, c0:c1])
 
         x_transpose(0)
+        x_out(0, nc.scalar.copy)
         w_grp = []
         for q in range(W_TILES // 2):
             bank = psum_s.tile([P, 2, 2, P], F32, name="wt", tag="s1")
@@ -224,54 +274,50 @@ def tile_moralinear_pa_t_kernel(tc, x, weight, lora_a_weight, out):
 
         def a_prepare():
             for jj in range(2):
-                bank = psum_s.tile([P, 2, 4, P], BF16, name="at", tag="s1")
+                bank = psum_o.tile([P, 2, 4, P], BF16, name="at", tag="o")
                 for j in range(2):
                     for s in range(4):
                         r0 = P * SLOT_TO_CHUNK[s]
                         nc.tensor.transpose(bank[:, j, s, :], a_raw[:, 2 * jj + j, r0 : r0 + P], ident_b[:])
-                nc.vector.tensor_copy(
+                nc.scalar.copy(
                     out=a_grp[:, 256 * jj : 256 * jj + 256, :].rearrange("p (j q) s -> p j q s", j=2),
                     in_=bank[:].rearrange("p j s q -> p j q s"),
                 )
 
         for hb in range(N_HB + 1):
-            first = hb < N_HB
-            second = hb >= 1
             prev = hb - 1
             tail = hb == N_HB
-            if second:
-                state[("o", prev)] = opool.tile([P, 2, OUT_DIM], F32, name="o_sb", tag="o_sb")
-            if hb + 1 < N_HB:
-                x_transpose(hb + 1)
-            if first:
-                new_half(hb)
-                plain_group(hb, 0)
-            if second:
-                z_quantise(prev, 2)
-                out_wide(prev, 0, 0, nc.scalar.copy)
-            if first:
-                plain_group(hb, 1)
-            if hb + 1 < N_HB:
-                x_quantise(hb + 1)
-            if second:
-                out_wide(prev, 1, 0, nc.vector.tensor_copy if tail else nc.scalar.copy)
+            other = nc.vector.tensor_copy if tail else nc.scalar.copy
+            plain_mm(hb, 0)
+            plain_mm(hb, 1)
+            x_transpose(hb + 1)
+            plain_out(hb, 0)
+            plain_out(hb, 1)
+            x_out(hb + 1, nc.vector.tensor_copy)
+            if hb == 1:
+                nc.vector.quantize_mx(out=a_codes[:].bitcast(FP8X4), scales=a_scales[:], in_=a_grp[:].rearrange("p q s -> p (q s)"))
+            z_quantise(prev, 1)
+            z_quantise(prev, 2)
+            z_quantise(hb, 0)
+            x_quantise(hb + 1)
+            out_wide(prev, 0, 0, nc.scalar.copy)
+            rotated(hb, 1, 0)
+            out_wide(prev, 1, 0, other)
+            if tail:
+                store(prev, 0, 512)
+            rotated(hb, 1, 1)
+            regroup(hb, 1)
+            rotated(hb, 2, 0)
+            out_wide(prev, 0, 1, nc.scalar.copy)
+            rotated(hb, 2, 1)
+            regroup(hb, 2)
             if hb == 0:
                 a_prepare()
-            if first:
-                rotated_pair(hb, 1, 0)
-                z_quantise(hb, 0)
-            if second:
-                out_wide(prev, 0, 1, nc.scalar.copy)
-            if first:
-                rotated_pair(hb, 1, 1)
-            if hb == 0:
-                nc.vector.quantize_mx(out=a_codes[:].bitcast(FP8X4), scales=a_scales[:], in_=a_grp[:].rearrange("p q s -> p (q s)"))
-            if second:
-                out_wide(prev, 1, 1, nc.vector.tensor_copy if tail else nc.scalar.copy)
-            if first:
-                rotated_pair(hb, 2, 0)
-                z_quantise(hb, 1)
-                rotated_pair(hb, 2, 1)
-            if second:
-                out_narrow(prev, nc.scalar.copy)
-                store(prev)
+            out_wide(prev, 1, 1, other)
+            if tail:
+                store(prev, 512, 1024)
+            out_narrow(prev, nc.scalar.copy)
+            if tail:
+                store(prev, 1024, 1280)
+            else:
+                store(prev, 0, 1280)

@@ -154,7 +154,7 @@ def tile_moralinear_pa_t_kernel(tc, x, weight, lora_a_weight, out):
             state[("g", hb, n)] = gpool.tile([P, HB, 4], BF16, name="zg%d" % n, tag="zg%d" % n, align_bytes=64)
             state[("zc", hb, n)] = zq.tile([P, HB], U32, name="zc%d" % n, tag="zc%d" % n, align_bytes=64)
             state[("zs", hb, n)] = zq.tile([P, HB], U8, name="zs%d" % n, tag="zs%d" % n, align_bytes=64)
-            if n > 0:
+            if n > 0 and hb < N_HB - 1:
                 state[("zp", hb, n)] = ppool.tile([P, 4, HB], BF16, name="zp%d" % n, tag="zp%d" % n)
 
         def plain_mm(hb, i):
@@ -176,7 +176,7 @@ def tile_moralinear_pa_t_kernel(tc, x, weight, lora_a_weight, out):
             t = slice(P * i, P * i + P)
             nc.vector.tensor_copy(out=state[("g", hb, 0)][:, t, :], in_=state[("g0", hb, i)][:].rearrange("p s t -> p t s"))
 
-        def rotated(hb, n, tm):
+        def rotated_mm(hb, n, tm):
             if not ok(hb):
                 return
             if tm == 0:
@@ -191,17 +191,34 @@ def tile_moralinear_pa_t_kernel(tc, x, weight, lora_a_weight, out):
             v = vpool.tile([P, 2, HB], F32, name="v", tag="v")
             nc.scalar.activation(out=v[:, 0, :], in_=bank[:, 1, :], func=ACT.Copy, scale=nsin_t[:, k : k + 1])
             nc.scalar.activation(out=v[:, 1, :], in_=bank[:, 0, :], func=ACT.Copy, scale=sin_t[:, k : k + 1])
-            nc.vector.scalar_tensor_tensor(
-                out=state[("zp", hb, n)][:, 2 * tm : 2 * tm + 2, :],
-                in0=bank[:],
-                scalar=cos_t[:, k : k + 1],
-                in1=v[:],
-                op0=ALU.mult,
-                op1=ALU.add,
-            )
+            state[("z", hb, n, tm)] = (bank, v)
+
+        def rotated_add(hb, n, tm):
+            if not ok(hb):
+                return
+            bank, v = state[("z", hb, n, tm)]
+            k = 2 * (n - 1) + tm
+            if hb == N_HB - 1:
+                nc.vector.scalar_tensor_tensor(
+                    out=state[("g", hb, n)][:, :, 2 * tm : 2 * tm + 2],
+                    in0=bank[:].rearrange("p a t -> p t a"),
+                    scalar=cos_t[:, k : k + 1],
+                    in1=v[:].rearrange("p a t -> p t a"),
+                    op0=ALU.mult,
+                    op1=ALU.add,
+                )
+            else:
+                nc.vector.scalar_tensor_tensor(
+                    out=state[("zp", hb, n)][:, 2 * tm : 2 * tm + 2, :],
+                    in0=bank[:],
+                    scalar=cos_t[:, k : k + 1],
+                    in1=v[:],
+                    op0=ALU.mult,
+                    op1=ALU.add,
+                )
 
         def regroup(hb, n):
-            if not ok(hb):
+            if not ok(hb) or hb == N_HB - 1:
                 return
             nc.gpsimd.tensor_scalar(
                 out=state[("g", hb, n)][:],
@@ -221,24 +238,25 @@ def tile_moralinear_pa_t_kernel(tc, x, weight, lora_a_weight, out):
                 in_=state[("g", hb, n)][:].rearrange("p t s -> p (t s)"),
             )
 
-        def out_wide(hb, i, c, copy):
+        def out_wide(hb, i, c, copy, pool):
             if not ok(hb):
                 return
-            if ("o", hb) not in state:
-                state[("o", hb)] = opool.tile([P, 2, OUT_DIM], F32, name="o_sb", tag="o_sb")
+            if i == 0:
+                state[("o", hb, c)] = opool.tile([P, 2, 512], F32, name="o_sb%d" % c, tag="o_sb%d" % c)
             xc, xs = state[("x", hb)]
             zc = state[("zc", hb, c)]
             zs = state[("zs", hb, c)]
             t = slice(P * i, P * i + P)
             cols = slice(512 * c, 512 * c + 512)
-            bank = psum_o.tile([P, 512], F32, name="o", tag="o")
+            bank = pool.tile([P, 512], F32, name="o", tag="o" if pool is psum_o else "s1")
             mx(bank[:], xc[:, t], xs[:, t], w_codes[:, cols], w_scales[:, cols], True, False)
             mx(bank[:], zc[:, t], zs[:, t], a_codes[:], a_scales[:], False, True)
-            copy(out=state[("o", hb)][:, i, cols], in_=bank[:])
+            copy(out=state[("o", hb, c)][:, i, :], in_=bank[:])
 
         def out_narrow(hb, copy):
             if not ok(hb):
                 return
+            state[("o", hb, 2)] = opool.tile([P, 2, 256], F32, name="o_sb2", tag="o_sb2")
             xc, xs = state[("x", hb)]
             zc = state[("zc", hb, 2)]
             zs = state[("zs", hb, 2)]
@@ -247,14 +265,14 @@ def tile_moralinear_pa_t_kernel(tc, x, weight, lora_a_weight, out):
                 t = slice(P * i, P * i + P)
                 mx(bank[:, i, :], xc[:, t], xs[:, t], w_codes[:, 1024:1280], w_scales[:, 1024:1280], True, False)
                 mx(bank[:, i, :], zc[:, t], zs[:, t], a_codes[:, 0:256], a_scales[:, 0:256], False, True)
-            copy(out=state[("o", hb)][:, :, 1024:1280], in_=bank[:])
+            copy(out=state[("o", hb, 2)][:], in_=bank[:])
 
-        def store(hb, c0, c1):
+        def store(hb, c):
             if not ok(hb):
                 return
             dst = out_blocks[hb // 2].rearrange("p (i c) -> p i c", i=4)
             h = hb % 2
-            nc.sync.dma_start(out=dst[:, 2 * h : 2 * h + 2, c0:c1], in_=state[("o", hb)][:, :, c0:c1])
+            nc.sync.dma_start(out=dst[:, 2 * h : 2 * h + 2, 512 * c : min(512 * c + 512, OUT_DIM)], in_=state[("o", hb, c)][:])
 
         x_transpose(0)
         x_out(0, nc.scalar.copy)
@@ -284,40 +302,49 @@ def tile_moralinear_pa_t_kernel(tc, x, weight, lora_a_weight, out):
                     in_=bank[:].rearrange("p j s q -> p j q s"),
                 )
 
-        for hb in range(N_HB + 1):
+        for hb in range(N_HB):
             prev = hb - 1
-            tail = hb == N_HB
-            other = nc.vector.tensor_copy if tail else nc.scalar.copy
             plain_mm(hb, 0)
             plain_mm(hb, 1)
             x_transpose(hb + 1)
+            rotated_mm(hb, 1, 0)
+            out_wide(prev, 0, 0, nc.scalar.copy, psum_o)
             plain_out(hb, 0)
             plain_out(hb, 1)
             x_out(hb + 1, nc.vector.tensor_copy)
-            if hb == 1:
-                nc.vector.quantize_mx(out=a_codes[:].bitcast(FP8X4), scales=a_scales[:], in_=a_grp[:].rearrange("p q s -> p (q s)"))
+            rotated_add(hb, 1, 0)
+            rotated_mm(hb, 1, 1)
+            if hb == 0:
+                a_prepare()
+            out_wide(prev, 1, 0, nc.scalar.copy, psum_o)
+            store(prev, 0)
             z_quantise(prev, 1)
             z_quantise(prev, 2)
             z_quantise(hb, 0)
             x_quantise(hb + 1)
-            out_wide(prev, 0, 0, nc.scalar.copy)
-            rotated(hb, 1, 0)
-            out_wide(prev, 1, 0, other)
-            if tail:
-                store(prev, 0, 512)
-            rotated(hb, 1, 1)
+            rotated_add(hb, 1, 1)
             regroup(hb, 1)
-            rotated(hb, 2, 0)
-            out_wide(prev, 0, 1, nc.scalar.copy)
-            rotated(hb, 2, 1)
+            rotated_mm(hb, 2, 0)
+            rotated_add(hb, 2, 0)
+            rotated_mm(hb, 2, 1)
+            out_wide(prev, 0, 1, nc.scalar.copy, psum_o)
+            rotated_add(hb, 2, 1)
             regroup(hb, 2)
             if hb == 0:
-                a_prepare()
-            out_wide(prev, 1, 1, other)
-            if tail:
-                store(prev, 512, 1024)
+                nc.vector.quantize_mx(out=a_codes[:].bitcast(FP8X4), scales=a_scales[:], in_=a_grp[:].rearrange("p q s -> p (q s)"))
+            out_wide(prev, 1, 1, nc.scalar.copy, psum_o)
+            store(prev, 1)
             out_narrow(prev, nc.scalar.copy)
-            if tail:
-                store(prev, 1024, 1280)
-            else:
-                store(prev, 0, 1280)
+            store(prev, 2)
+
+        last = N_HB - 1
+        z_quantise(last, 1)
+        z_quantise(last, 2)
+        out_wide(last, 0, 0, nc.vector.tensor_copy, psum_o)
+        out_wide(last, 1, 0, nc.scalar.copy, psum_o)
+        store(last, 0)
+        out_wide(last, 0, 1, nc.vector.tensor_copy, psum_s)
+        out_wide(last, 1, 1, nc.scalar.copy, psum_s)
+        store(last, 1)
+        out_narrow(last, nc.vector.tensor_copy)
+        store(last, 2)

@@ -40,15 +40,16 @@ def tile_moralinear_pa_t_kernel(tc, x, weight, lora_a_weight, out):
         const = ctx.enter_context(tc.tile_pool(name="const", bufs=1))
         xin = ctx.enter_context(tc.tile_pool(name="xin", bufs=8))
         win = ctx.enter_context(tc.tile_pool(name="win", bufs=5))
-        grp = ctx.enter_context(tc.tile_pool(name="grp", bufs=3))
-        xq = ctx.enter_context(tc.tile_pool(name="xq", bufs=5))
+        grp = ctx.enter_context(tc.tile_pool(name="grp", bufs=5))
+        xq = ctx.enter_context(tc.tile_pool(name="xq", bufs=6))
         vpool = ctx.enter_context(tc.tile_pool(name="vpool", bufs=4))
         gpool = ctx.enter_context(tc.tile_pool(name="gpool", bufs=3))
         ppool = ctx.enter_context(tc.tile_pool(name="ppool", bufs=3))
         zq = ctx.enter_context(tc.tile_pool(name="zq", bufs=3))
         opool = ctx.enter_context(tc.tile_pool(name="opool", bufs=3))
-        psum_x = ctx.enter_context(tc.psum_pool(name="psum_x", bufs=1))
-        psum_s = ctx.enter_context(tc.psum_pool(name="psum_s", bufs=4))
+        psum_p = ctx.enter_context(tc.psum_pool(name="psum_p", bufs=2))
+        psum_r = ctx.enter_context(tc.psum_pool(name="psum_r", bufs=2))
+        psum_c = ctx.enter_context(tc.psum_pool(name="psum_c", bufs=1))
         psum_o = ctx.enter_context(tc.psum_pool(name="psum_o", bufs=3))
         if PIN:
             ctx.enter_context(tc.manual_schedule())
@@ -56,12 +57,14 @@ def tile_moralinear_pa_t_kernel(tc, x, weight, lora_a_weight, out):
         x_raw = []
         w_raw = []
         xr0 = xin.tile([P, 4 * IN_DIM], BF16, name="x_raw", tag="x_raw")
-        nc.sync.dma_start(out=xr0[:], in_=x_blocks[0])
         x_raw.append(xr0)
         for q in range(W_TILES // 2):
             wr = win.tile([P, 2, IN_DIM], BF16, name="w_raw", tag="w_raw")
             nc.sync.dma_start(out=wr[:], in_=w_pairs[q])
             w_raw.append(wr)
+            if q == 0:
+                nc.sync.dma_start(out=xr0[:, : 2 * IN_DIM], in_=x_blocks[0][:, : 2 * IN_DIM])
+        nc.sync.dma_start(out=xr0[:, 2 * IN_DIM :], in_=x_blocks[0][:, 2 * IN_DIM :])
         a_raw = const.tile([P, 4, R], BF16)
         nc.sync.dma_start(out=a_raw[:], in_=a_rows)
         for b in range(1, TOKENS // 512):
@@ -93,6 +96,10 @@ def tile_moralinear_pa_t_kernel(tc, x, weight, lora_a_weight, out):
         nc.vector.tensor_tensor(out=sq_t[:], in0=half_t[:], in1=half_t[:], op=ALU.mult)
         cos_t = const.tile([P, 4], F32)
         nc.vector.tensor_scalar(out=cos_t[:], in0=sq_t[:], scalar1=-2.0, scalar2=1.0, op0=ALU.mult, op1=ALU.add)
+
+        cot_t = const.tile([P, 4], F32)
+        nc.vector.reciprocal(out=cot_t[:], in_=nsin_t[:])
+        nc.vector.tensor_tensor(out=cot_t[:], in0=cot_t[:], in1=cos_t[:], op=ALU.mult)
 
         w_codes = const.tile([P, OUT_DIM], U32, align_bytes=64)
         w_scales = const.tile([P, OUT_DIM], U8, align_bytes=64)
@@ -131,7 +138,7 @@ def tile_moralinear_pa_t_kernel(tc, x, weight, lora_a_weight, out):
         def x_transpose(hb):
             if not ok(hb):
                 return
-            bank = psum_x.tile([P, 2, 2, P], F32, name="xt", tag="xt")
+            bank = psum_o.tile([P, 2, 2, P], F32, name="xt", tag="o")
             word_transposes(bank, x_raw[hb // 2][:].bitcast(F32), 512 * (hb % 2))
             state[("xt", hb)] = bank
 
@@ -163,7 +170,7 @@ def tile_moralinear_pa_t_kernel(tc, x, weight, lora_a_weight, out):
             if i == 0:
                 new_group(hb, 0)
             xc, xs = state[("x", hb)]
-            bank = psum_s.tile([P, 4, P], F32, name="g0", tag="s1")
+            bank = psum_p.tile([P, 4, P], F32, name="g0", tag="p")
             t = slice(P * i, P * i + P)
             for s in range(4):
                 w = slice(P * SLOT_TO_CHUNK[s], P * SLOT_TO_CHUNK[s] + P)
@@ -176,29 +183,56 @@ def tile_moralinear_pa_t_kernel(tc, x, weight, lora_a_weight, out):
             t = slice(P * i, P * i + P)
             nc.vector.tensor_copy(out=state[("g", hb, 0)][:, t, :], in_=state[("g0", hb, i)][:].rearrange("p s t -> p t s"))
 
-        def rotated_mm(hb, n, tm):
+        def rotated_mm(hb, n, tm, pool=psum_r, tag="r"):
             if not ok(hb):
                 return
             if tm == 0:
                 new_group(hb, n)
             xc, xs = state[("x", hb)]
-            bank = psum_s.tile([P, 2, HB], F32, name="z", tag="s1")
+            bank = pool.tile([P, 2, HB], F32, name="z", tag=tag)
+            state[("z", hb, n, tm)] = bank
             for ab in range(2):
                 jw = (4 * n + tm + 2 * ab) % W_TILES
                 w = slice(P * jw, P * jw + P)
                 mx(bank[:, ab, :], w_codes[:, w], w_scales[:, w], xc[:], xs[:], True, True)
+
+        def on_gpsimd(hb, n, tm):
+            return tm == 0 and n == 1 and hb < N_HB - 1
+
+        def rotated_w(hb, n, tm):
+            if not ok(hb) or not on_gpsimd(hb, n, tm):
+                return
+            v = state[("v", hb, n, tm)]
+            k = 2 * (n - 1) + tm
+            nc.gpsimd.tensor_scalar(out=v[:, 1, :], in0=v[:, 0, :], scalar1=cot_t[:, k : k + 1], scalar2=0.0, op0=ALU.mult, op1=ALU.add)
+
+        def rotated_v(hb, n, tm):
+            if not ok(hb):
+                return
+            bank = state[("z", hb, n, tm)]
             k = 2 * (n - 1) + tm
             v = vpool.tile([P, 2, HB], F32, name="v", tag="v")
             nc.scalar.activation(out=v[:, 0, :], in_=bank[:, 1, :], func=ACT.Copy, scale=nsin_t[:, k : k + 1])
-            nc.scalar.activation(out=v[:, 1, :], in_=bank[:, 0, :], func=ACT.Copy, scale=sin_t[:, k : k + 1])
-            state[("z", hb, n, tm)] = (bank, v)
+            if not on_gpsimd(hb, n, tm):
+                nc.scalar.activation(out=v[:, 1, :], in_=bank[:, 0, :], func=ACT.Copy, scale=sin_t[:, k : k + 1])
+            state[("v", hb, n, tm)] = v
 
         def rotated_add(hb, n, tm):
             if not ok(hb):
                 return
-            bank, v = state[("z", hb, n, tm)]
+            bank, v = state[("z", hb, n, tm)], state[("v", hb, n, tm)]
             k = 2 * (n - 1) + tm
-            if hb == N_HB - 1:
+            if on_gpsimd(hb, n, tm):
+                for half, scale in enumerate((cos_t, sin_t)):
+                    nc.vector.scalar_tensor_tensor(
+                        out=state[("zp", hb, n)][:, 2 * tm + half, :],
+                        in0=bank[:, 0, :],
+                        scalar=scale[:, k : k + 1],
+                        in1=v[:, half, :],
+                        op0=ALU.mult,
+                        op1=ALU.add,
+                    )
+            elif hb == N_HB - 1:
                 nc.vector.scalar_tensor_tensor(
                     out=state[("g", hb, n)][:, :, 2 * tm : 2 * tm + 2],
                     in0=bank[:].rearrange("p a t -> p t a"),
@@ -216,6 +250,63 @@ def tile_moralinear_pa_t_kernel(tc, x, weight, lora_a_weight, out):
                     op0=ALU.mult,
                     op1=ALU.add,
                 )
+
+        def second_mm(hb):
+            if not ok(hb) or hb == N_HB - 1:
+                return
+            xc, xs = state[("x", hb)]
+            new_group(hb, 2)
+            bank = psum_c.tile([P, 2, HB], F32, name="zc", tag="c")
+            for tm in range(2):
+                w = slice(P * (8 + tm), P * (8 + tm) + P)
+                mx(bank[:, tm, :], w_codes[:, w], w_scales[:, w], xc[:], xs[:], True, True)
+            state[("c", hb)] = bank
+
+        def second_v(hb):
+            if not ok(hb) or hb == N_HB - 1:
+                return
+            v = vpool.tile([P, 2, HB], F32, name="v2", tag="v2")
+            for i in range(2):
+                for tm in range(2):
+                    nc.scalar.activation(
+                        out=v[:, tm, P * i : P * i + P],
+                        in_=state[("g0", hb, i)][:, 2 * tm, :],
+                        func=ACT.Copy,
+                        scale=nsin_t[:, 2 + tm : 3 + tm],
+                    )
+            state[("v2", hb)] = v
+
+        def second_w(hb):
+            if not ok(hb) or hb == N_HB - 1:
+                return
+            v = state[("v2", hb)]
+            w2 = vpool.tile([P, 2, HB], F32, name="w2", tag="w2")
+            for tm in range(2):
+                nc.gpsimd.tensor_scalar(
+                    out=w2[:, tm, :],
+                    in0=v[:, tm, :],
+                    scalar1=cot_t[:, 2 + tm : 3 + tm],
+                    scalar2=0.0,
+                    op0=ALU.mult,
+                    op1=ALU.add,
+                )
+            state[("w2", hb)] = w2
+
+        def second_add(hb):
+            if not ok(hb) or hb == N_HB - 1:
+                return
+            bank = state[("c", hb)]
+            zp = state[("zp", hb, 2)]
+            for half, (scale, other) in enumerate(((cos_t, "v2"), (sin_t, "w2"))):
+                for tm in range(2):
+                    nc.vector.scalar_tensor_tensor(
+                        out=zp[:, 2 * tm + half, :],
+                        in0=bank[:, tm, :],
+                        scalar=scale[:, 2 + tm : 3 + tm],
+                        in1=state[(other, hb)][:, tm, :],
+                        op0=ALU.mult,
+                        op1=ALU.add,
+                    )
 
         def regroup(hb, n):
             if not ok(hb) or hb == N_HB - 1:
@@ -248,7 +339,7 @@ def tile_moralinear_pa_t_kernel(tc, x, weight, lora_a_weight, out):
             zs = state[("zs", hb, c)]
             t = slice(P * i, P * i + P)
             cols = slice(512 * c, 512 * c + 512)
-            bank = pool.tile([P, 512], F32, name="o", tag="o" if pool is psum_o else "s1")
+            bank = pool.tile([P, 512], F32, name="o", tag="o" if pool is psum_o else "p" if pool is psum_p else "r")
             mx(bank[:], xc[:, t], xs[:, t], w_codes[:, cols], w_scales[:, cols], True, False)
             mx(bank[:], zc[:, t], zs[:, t], a_codes[:], a_scales[:], False, True)
             copy(out=state[("o", hb, c)][:, i, :], in_=bank[:])
@@ -274,21 +365,41 @@ def tile_moralinear_pa_t_kernel(tc, x, weight, lora_a_weight, out):
             h = hb % 2
             nc.sync.dma_start(out=dst[:, 2 * h : 2 * h + 2, 512 * c : min(512 * c + 512, OUT_DIM)], in_=state[("o", hb, c)][:])
 
-        x_transpose(0)
-        x_out(0, nc.scalar.copy)
-        w_grp = []
-        for q in range(W_TILES // 2):
-            bank = psum_s.tile([P, 2, 2, P], F32, name="wt", tag="s1")
+        w_grp = {}
+
+        def w_transpose(q, copy, pool, tag):
+            bank = pool.tile([P, 2, 2, P], F32, name="wt", tag=tag)
             word_transposes(bank, w_raw[q][:].rearrange("p j k -> p (j k)").bitcast(F32), 0)
             wg = grp.tile([P, 4 * 256], BF16, name="wg", tag="wg", align_bytes=64)
-            words_out(nc.vector.tensor_copy if q % 2 == 0 else nc.scalar.copy, wg, bank)
-            w_grp.append(wg)
-            if q == 0:
-                x_quantise(0)
-            if q >= 1:
-                cols = slice(256 * (q - 1), 256 * q)
-                nc.vector.quantize_mx(out=w_codes[:, cols].bitcast(FP8X4), scales=w_scales[:, cols], in_=w_grp[q - 1][:])
-        nc.vector.quantize_mx(out=w_codes[:, 1024:1280].bitcast(FP8X4), scales=w_scales[:, 1024:1280], in_=w_grp[4][:])
+            words_out(copy, wg, bank)
+            w_grp[q] = wg
+
+        def w_quantise(q):
+            cols = slice(256 * q, 256 * q + 256)
+            nc.vector.quantize_mx(out=w_codes[:, cols].bitcast(FP8X4), scales=w_scales[:, cols], in_=w_grp[q][:])
+
+        w_transpose(0, nc.vector.tensor_copy, psum_p, "p")
+        x_transpose(0)
+        x_out(0, nc.scalar.copy)
+        w_transpose(1, nc.scalar.copy, psum_p, "p")
+        w_quantise(0)
+        w_transpose(2, nc.vector.tensor_copy, psum_r, "r")
+        x_quantise(0)
+        w_quantise(1)
+        w_transpose(3, nc.scalar.copy, psum_r, "r")
+        w_quantise(2)
+        w_transpose(4, nc.scalar.copy, psum_c, "c")
+        plain_mm(0, 0)
+        plain_mm(0, 1)
+        w_quantise(3)
+        rotated_mm(0, 1, 0)
+        rotated_mm(0, 1, 1)
+        x_transpose(1)
+        rotated_v(0, 1, 0)
+        rotated_w(0, 1, 0)
+        rotated_v(0, 1, 1)
+        x_out(1, nc.scalar.copy)
+        w_quantise(4)
 
         def a_prepare():
             for jj in range(2):
@@ -302,49 +413,74 @@ def tile_moralinear_pa_t_kernel(tc, x, weight, lora_a_weight, out):
                     in_=bank[:].rearrange("p j s q -> p j q s"),
                 )
 
-        for hb in range(N_HB):
+        for hb in range(N_HB - 1):
             prev = hb - 1
-            plain_mm(hb, 0)
-            plain_mm(hb, 1)
-            x_transpose(hb + 1)
-            rotated_mm(hb, 1, 0)
-            out_wide(prev, 0, 0, nc.scalar.copy, psum_o)
             plain_out(hb, 0)
             plain_out(hb, 1)
-            x_out(hb + 1, nc.vector.tensor_copy)
-            rotated_add(hb, 1, 0)
-            rotated_mm(hb, 1, 1)
             if hb == 0:
                 a_prepare()
-            out_wide(prev, 1, 0, nc.scalar.copy, psum_o)
-            store(prev, 0)
+            second_v(hb)
+            second_w(hb)
+            second_mm(hb)
+            out_wide(prev, 0, 0, nc.scalar.copy, psum_o)
+            rotated_add(hb, 1, 0)
+            x_quantise(hb + 1)
+            z_quantise(hb, 0)
             z_quantise(prev, 1)
             z_quantise(prev, 2)
-            z_quantise(hb, 0)
-            x_quantise(hb + 1)
+            out_wide(prev, 1, 0, nc.scalar.copy, psum_o)
+            store(prev, 0)
+            x_transpose(hb + 2)
+            x_out(hb + 2, nc.scalar.copy)
             rotated_add(hb, 1, 1)
             regroup(hb, 1)
-            rotated_mm(hb, 2, 0)
-            rotated_add(hb, 2, 0)
-            rotated_mm(hb, 2, 1)
+            plain_mm(hb + 1, 0)
+            plain_mm(hb + 1, 1)
             out_wide(prev, 0, 1, nc.scalar.copy, psum_o)
-            rotated_add(hb, 2, 1)
+            rotated_mm(hb + 1, 1, 0)
+            rotated_v(hb + 1, 1, 0)
+            out_wide(prev, 1, 1, nc.scalar.copy, psum_o)
+            store(prev, 1)
+            second_add(hb)
+            rotated_w(hb + 1, 1, 0)
             regroup(hb, 2)
             if hb == 0:
                 nc.vector.quantize_mx(out=a_codes[:].bitcast(FP8X4), scales=a_scales[:], in_=a_grp[:].rearrange("p q s -> p (q s)"))
-            out_wide(prev, 1, 1, nc.scalar.copy, psum_o)
-            store(prev, 1)
+            rotated_mm(hb + 1, 1, 1)
+            rotated_v(hb + 1, 1, 1)
             out_narrow(prev, nc.scalar.copy)
             store(prev, 2)
 
         last = N_HB - 1
+        prev = last - 1
+        rotated_mm(last, 2, 0, psum_c, "c")
+        rotated_v(last, 2, 0)
+        plain_out(last, 0)
+        plain_out(last, 1)
+        out_wide(prev, 0, 0, nc.scalar.copy, psum_o)
+        rotated_mm(last, 2, 1, psum_p, "p")
+        rotated_v(last, 2, 1)
+        rotated_add(last, 1, 0)
+        z_quantise(last, 0)
+        z_quantise(prev, 1)
+        z_quantise(prev, 2)
+        out_wide(prev, 1, 0, nc.scalar.copy, psum_o)
+        store(prev, 0)
+        rotated_add(last, 1, 1)
+        out_wide(prev, 0, 1, nc.scalar.copy, psum_o)
+        out_wide(prev, 1, 1, nc.scalar.copy, psum_o)
+        store(prev, 1)
+        rotated_add(last, 2, 0)
         z_quantise(last, 1)
-        z_quantise(last, 2)
-        out_wide(last, 0, 0, nc.vector.tensor_copy, psum_o)
-        out_wide(last, 1, 0, nc.scalar.copy, psum_o)
+        out_narrow(prev, nc.scalar.copy)
+        store(prev, 2)
+        rotated_add(last, 2, 1)
+        out_wide(last, 0, 0, nc.scalar.copy, psum_r)
+        out_wide(last, 1, 0, nc.scalar.copy, psum_r)
         store(last, 0)
-        out_wide(last, 0, 1, nc.vector.tensor_copy, psum_s)
-        out_wide(last, 1, 1, nc.scalar.copy, psum_s)
+        z_quantise(last, 2)
+        out_wide(last, 0, 1, nc.vector.tensor_copy, psum_o)
+        out_wide(last, 1, 1, nc.scalar.copy, psum_p)
         store(last, 1)
         out_narrow(last, nc.vector.tensor_copy)
         store(last, 2)

@@ -196,16 +196,6 @@ def tile_moralinear_pa_t_kernel(tc, x, weight, lora_a_weight, out):
                 w = slice(P * jw, P * jw + P)
                 mx(bank[:, ab, :], w_codes[:, w], w_scales[:, w], xc[:], xs[:], True, True)
 
-        def on_gpsimd(hb, n, tm):
-            return tm == 0 and n == 1 and hb < N_HB - 1
-
-        def rotated_w(hb, n, tm):
-            if not ok(hb) or not on_gpsimd(hb, n, tm):
-                return
-            v = state[("v", hb, n, tm)]
-            k = 2 * (n - 1) + tm
-            nc.gpsimd.tensor_scalar(out=v[:, 1, :], in0=v[:, 0, :], scalar1=cot_t[:, k : k + 1], scalar2=0.0, op0=ALU.mult, op1=ALU.add)
-
         def rotated_v(hb, n, tm):
             if not ok(hb):
                 return
@@ -213,8 +203,7 @@ def tile_moralinear_pa_t_kernel(tc, x, weight, lora_a_weight, out):
             k = 2 * (n - 1) + tm
             v = vpool.tile([P, 2, HB], F32, name="v", tag="v")
             nc.scalar.activation(out=v[:, 0, :], in_=bank[:, 1, :], func=ACT.Copy, scale=nsin_t[:, k : k + 1])
-            if not on_gpsimd(hb, n, tm):
-                nc.scalar.activation(out=v[:, 1, :], in_=bank[:, 0, :], func=ACT.Copy, scale=sin_t[:, k : k + 1])
+            nc.scalar.activation(out=v[:, 1, :], in_=bank[:, 0, :], func=ACT.Copy, scale=sin_t[:, k : k + 1])
             state[("v", hb, n, tm)] = v
 
         def rotated_add(hb, n, tm):
@@ -222,17 +211,7 @@ def tile_moralinear_pa_t_kernel(tc, x, weight, lora_a_weight, out):
                 return
             bank, v = state[("z", hb, n, tm)], state[("v", hb, n, tm)]
             k = 2 * (n - 1) + tm
-            if on_gpsimd(hb, n, tm):
-                for half, scale in enumerate((cos_t, sin_t)):
-                    nc.vector.scalar_tensor_tensor(
-                        out=state[("zp", hb, n)][:, 2 * tm + half, :],
-                        in0=bank[:, 0, :],
-                        scalar=scale[:, k : k + 1],
-                        in1=v[:, half, :],
-                        op0=ALU.mult,
-                        op1=ALU.add,
-                    )
-            elif hb == N_HB - 1:
+            if hb == N_HB - 1:
                 nc.vector.scalar_tensor_tensor(
                     out=state[("g", hb, n)][:, :, 2 * tm : 2 * tm + 2],
                     in0=bank[:].rearrange("p a t -> p t a"),
@@ -276,13 +255,13 @@ def tile_moralinear_pa_t_kernel(tc, x, weight, lora_a_weight, out):
                     )
             state[("v2", hb)] = v
 
-        def second_w(hb):
+        def second_w(hb, engine=nc.vector):
             if not ok(hb) or hb == N_HB - 1:
                 return
             v = state[("v2", hb)]
             w2 = vpool.tile([P, 2, HB], F32, name="w2", tag="w2")
             for tm in range(2):
-                nc.gpsimd.tensor_scalar(
+                engine.tensor_scalar(
                     out=w2[:, tm, :],
                     in0=v[:, tm, :],
                     scalar1=cot_t[:, 2 + tm : 3 + tm],
@@ -344,7 +323,7 @@ def tile_moralinear_pa_t_kernel(tc, x, weight, lora_a_weight, out):
             mx(bank[:], zc[:, t], zs[:, t], a_codes[:], a_scales[:], False, True)
             copy(out=state[("o", hb, c)][:, i, :], in_=bank[:])
 
-        def out_narrow(hb, copy):
+        def narrow_mm(hb):
             if not ok(hb):
                 return
             state[("o", hb, 2)] = opool.tile([P, 2, 256], F32, name="o_sb2", tag="o_sb2")
@@ -356,7 +335,12 @@ def tile_moralinear_pa_t_kernel(tc, x, weight, lora_a_weight, out):
                 t = slice(P * i, P * i + P)
                 mx(bank[:, i, :], xc[:, t], xs[:, t], w_codes[:, 1024:1280], w_scales[:, 1024:1280], True, False)
                 mx(bank[:, i, :], zc[:, t], zs[:, t], a_codes[:, 0:256], a_scales[:, 0:256], False, True)
-            copy(out=state[("o", hb, 2)][:], in_=bank[:])
+            state[("n", hb)] = bank
+
+        def narrow_out(hb, copy):
+            if not ok(hb):
+                return
+            copy(out=state[("o", hb, 2)][:], in_=state[("n", hb)][:])
 
         def store(hb, c):
             if not ok(hb):
@@ -393,11 +377,8 @@ def tile_moralinear_pa_t_kernel(tc, x, weight, lora_a_weight, out):
         plain_mm(0, 1)
         w_quantise(3)
         rotated_mm(0, 1, 0)
-        rotated_mm(0, 1, 1)
         x_transpose(1)
         rotated_v(0, 1, 0)
-        rotated_w(0, 1, 0)
-        rotated_v(0, 1, 1)
         x_out(1, nc.scalar.copy)
         w_quantise(4)
 
@@ -417,46 +398,48 @@ def tile_moralinear_pa_t_kernel(tc, x, weight, lora_a_weight, out):
             prev = hb - 1
             plain_out(hb, 0)
             plain_out(hb, 1)
+            second_v(hb)
+            rotated_mm(hb, 1, 1)
+            rotated_v(hb, 1, 1)
+            second_mm(hb)
             if hb == 0:
                 a_prepare()
-            second_v(hb)
-            second_w(hb)
-            second_mm(hb)
-            out_wide(prev, 0, 0, nc.scalar.copy, psum_o)
             rotated_add(hb, 1, 0)
-            x_quantise(hb + 1)
-            z_quantise(hb, 0)
-            z_quantise(prev, 1)
-            z_quantise(prev, 2)
+            out_wide(prev, 0, 0, nc.scalar.copy, psum_o)
             out_wide(prev, 1, 0, nc.scalar.copy, psum_o)
             store(prev, 0)
             x_transpose(hb + 2)
             x_out(hb + 2, nc.scalar.copy)
-            rotated_add(hb, 1, 1)
-            regroup(hb, 1)
+            x_quantise(hb + 1)
+            z_quantise(hb, 0)
+            z_quantise(prev, 1)
+            z_quantise(prev, 2)
             plain_mm(hb + 1, 0)
             plain_mm(hb + 1, 1)
-            out_wide(prev, 0, 1, nc.scalar.copy, psum_o)
+            rotated_add(hb, 1, 1)
+            regroup(hb, 1)
+            second_w(hb)
             rotated_mm(hb + 1, 1, 0)
             rotated_v(hb + 1, 1, 0)
+            out_wide(prev, 0, 1, nc.scalar.copy, psum_o)
             out_wide(prev, 1, 1, nc.scalar.copy, psum_o)
             store(prev, 1)
+            narrow_mm(prev)
+            narrow_out(prev, nc.scalar.copy)
+            store(prev, 2)
             second_add(hb)
-            rotated_w(hb + 1, 1, 0)
             regroup(hb, 2)
             if hb == 0:
                 nc.vector.quantize_mx(out=a_codes[:].bitcast(FP8X4), scales=a_scales[:], in_=a_grp[:].rearrange("p q s -> p (q s)"))
-            rotated_mm(hb + 1, 1, 1)
-            rotated_v(hb + 1, 1, 1)
-            out_narrow(prev, nc.scalar.copy)
-            store(prev, 2)
 
         last = N_HB - 1
         prev = last - 1
         rotated_mm(last, 2, 0, psum_c, "c")
-        rotated_v(last, 2, 0)
+        rotated_mm(last, 1, 1)
         plain_out(last, 0)
         plain_out(last, 1)
+        rotated_v(last, 1, 1)
+        rotated_v(last, 2, 0)
         out_wide(prev, 0, 0, nc.scalar.copy, psum_o)
         rotated_mm(last, 2, 1, psum_p, "p")
         rotated_v(last, 2, 1)
@@ -472,7 +455,8 @@ def tile_moralinear_pa_t_kernel(tc, x, weight, lora_a_weight, out):
         store(prev, 1)
         rotated_add(last, 2, 0)
         z_quantise(last, 1)
-        out_narrow(prev, nc.scalar.copy)
+        narrow_mm(prev)
+        narrow_out(prev, nc.scalar.copy)
         store(prev, 2)
         rotated_add(last, 2, 1)
         out_wide(last, 0, 0, nc.scalar.copy, psum_r)
@@ -482,5 +466,6 @@ def tile_moralinear_pa_t_kernel(tc, x, weight, lora_a_weight, out):
         out_wide(last, 0, 1, nc.vector.tensor_copy, psum_o)
         out_wide(last, 1, 1, nc.scalar.copy, psum_p)
         store(last, 1)
-        out_narrow(last, nc.vector.tensor_copy)
+        narrow_mm(last)
+        narrow_out(last, nc.vector.tensor_copy)
         store(last, 2)

@@ -108,6 +108,10 @@ def tile_moralinear_pa_t_kernel(tc, x, weight, lora_a_weight, out):
         a_grp = const.tile([P, R, 4], BF16, align_bytes=64)
 
         state = {}
+        tags = ((psum_p, "p"), (psum_r, "r"), (psum_c, "c"), (psum_o, "o"))
+
+        def tag_of(pool):
+            return [tag for known, tag in tags if known is pool][0]
 
         def ok(hb):
             return 0 <= hb < N_HB
@@ -241,19 +245,23 @@ def tile_moralinear_pa_t_kernel(tc, x, weight, lora_a_weight, out):
                 mx(bank[:, tm, :], w_codes[:, w], w_scales[:, w], xc[:], xs[:], True, True)
             state[("c", hb)] = bank
 
-        def second_v(hb):
+        def second_v_part(hb, i, tm, engine):
             if not ok(hb) or hb == N_HB - 1:
                 return
-            v = vpool.tile([P, 2, HB], F32, name="v2", tag="v2")
+            if ("v2", hb) not in state:
+                state[("v2", hb)] = vpool.tile([P, 2, HB], F32, name="v2", tag="v2")
+            out = state[("v2", hb)][:, tm, P * i : P * i + P]
+            src = state[("g0", hb, i)][:, 2 * tm, :]
+            scale = nsin_t[:, 2 + tm : 3 + tm]
+            if engine is nc.scalar:
+                nc.scalar.activation(out=out, in_=src, func=ACT.Copy, scale=scale)
+            else:
+                nc.vector.tensor_scalar(out=out, in0=src, scalar1=scale, scalar2=None, op0=ALU.mult)
+
+        def second_v(hb):
             for i in range(2):
                 for tm in range(2):
-                    nc.scalar.activation(
-                        out=v[:, tm, P * i : P * i + P],
-                        in_=state[("g0", hb, i)][:, 2 * tm, :],
-                        func=ACT.Copy,
-                        scale=nsin_t[:, 2 + tm : 3 + tm],
-                    )
-            state[("v2", hb)] = v
+                    second_v_part(hb, i, tm, nc.scalar)
 
         def second_w(hb, engine=nc.vector):
             if not ok(hb) or hb == N_HB - 1:
@@ -318,19 +326,19 @@ def tile_moralinear_pa_t_kernel(tc, x, weight, lora_a_weight, out):
             zs = state[("zs", hb, c)]
             t = slice(P * i, P * i + P)
             cols = slice(512 * c, 512 * c + 512)
-            bank = pool.tile([P, 512], F32, name="o", tag="o" if pool is psum_o else "p" if pool is psum_p else "r")
+            bank = pool.tile([P, 512], F32, name="o", tag=tag_of(pool))
             mx(bank[:], xc[:, t], xs[:, t], w_codes[:, cols], w_scales[:, cols], True, False)
             mx(bank[:], zc[:, t], zs[:, t], a_codes[:], a_scales[:], False, True)
             copy(out=state[("o", hb, c)][:, i, :], in_=bank[:])
 
-        def narrow_mm(hb):
+        def narrow_mm(hb, pool=psum_o):
             if not ok(hb):
                 return
             state[("o", hb, 2)] = opool.tile([P, 2, 256], F32, name="o_sb2", tag="o_sb2")
             xc, xs = state[("x", hb)]
             zc = state[("zc", hb, 2)]
             zs = state[("zs", hb, 2)]
-            bank = psum_o.tile([P, 2, 256], F32, name="o2", tag="o")
+            bank = pool.tile([P, 2, 256], F32, name="o2", tag=tag_of(pool))
             for i in range(2):
                 t = slice(P * i, P * i + P)
                 mx(bank[:, i, :], xc[:, t], xs[:, t], w_codes[:, 1024:1280], w_scales[:, 1024:1280], True, False)
@@ -341,6 +349,16 @@ def tile_moralinear_pa_t_kernel(tc, x, weight, lora_a_weight, out):
             if not ok(hb):
                 return
             copy(out=state[("o", hb, 2)][:], in_=state[("n", hb)][:])
+
+        def narrow_half(hb, i, copy):
+            copy(out=state[("o", hb, 2)][:, i, :], in_=state[("n", hb)][:, i, :])
+
+        def store_half(hb, c, i):
+            dst = out_blocks[hb // 2].rearrange("p (i c) -> p i c", i=4)
+            nc.sync.dma_start(
+                out=dst[:, 2 * (hb % 2) + i, 512 * c : min(512 * c + 512, OUT_DIM)],
+                in_=state[("o", hb, c)][:, i, :],
+            )
 
         def store(hb, c):
             if not ok(hb):
@@ -373,13 +391,13 @@ def tile_moralinear_pa_t_kernel(tc, x, weight, lora_a_weight, out):
         w_transpose(3, nc.scalar.copy, psum_r, "r")
         w_quantise(2)
         w_transpose(4, nc.scalar.copy, psum_c, "c")
+        x_transpose(1)
+        x_out(1, nc.scalar.copy)
         plain_mm(0, 0)
         plain_mm(0, 1)
         w_quantise(3)
         rotated_mm(0, 1, 0)
-        x_transpose(1)
         rotated_v(0, 1, 0)
-        x_out(1, nc.scalar.copy)
         w_quantise(4)
 
         def a_prepare():
@@ -398,7 +416,10 @@ def tile_moralinear_pa_t_kernel(tc, x, weight, lora_a_weight, out):
             prev = hb - 1
             plain_out(hb, 0)
             plain_out(hb, 1)
-            second_v(hb)
+            second_v_part(hb, 1, 1, nc.vector)
+            second_v_part(hb, 0, 0, nc.scalar)
+            second_v_part(hb, 0, 1, nc.scalar)
+            second_v_part(hb, 1, 0, nc.scalar)
             rotated_mm(hb, 1, 1)
             rotated_v(hb, 1, 1)
             second_mm(hb)
@@ -441,31 +462,35 @@ def tile_moralinear_pa_t_kernel(tc, x, weight, lora_a_weight, out):
         rotated_v(last, 1, 1)
         rotated_v(last, 2, 0)
         out_wide(prev, 0, 0, nc.scalar.copy, psum_o)
+        store_half(prev, 0, 0)
         rotated_mm(last, 2, 1, psum_p, "p")
-        rotated_v(last, 2, 1)
         rotated_add(last, 1, 0)
         z_quantise(last, 0)
         z_quantise(prev, 1)
         z_quantise(prev, 2)
         out_wide(prev, 1, 0, nc.scalar.copy, psum_o)
-        store(prev, 0)
+        store_half(prev, 0, 1)
+        rotated_v(last, 2, 1)
         rotated_add(last, 1, 1)
         out_wide(prev, 0, 1, nc.scalar.copy, psum_o)
-        out_wide(prev, 1, 1, nc.scalar.copy, psum_o)
-        store(prev, 1)
+        store_half(prev, 1, 0)
+        out_wide(prev, 1, 1, nc.scalar.copy, psum_p)
+        store_half(prev, 1, 1)
         rotated_add(last, 2, 0)
         z_quantise(last, 1)
-        narrow_mm(prev)
+        narrow_mm(prev, psum_r)
         narrow_out(prev, nc.scalar.copy)
         store(prev, 2)
         rotated_add(last, 2, 1)
-        out_wide(last, 0, 0, nc.scalar.copy, psum_r)
-        out_wide(last, 1, 0, nc.scalar.copy, psum_r)
-        store(last, 0)
+        out_wide(last, 0, 0, nc.scalar.copy, psum_o)
+        store_half(last, 0, 0)
+        out_wide(last, 1, 0, nc.scalar.copy, psum_o)
+        store_half(last, 0, 1)
         z_quantise(last, 2)
         out_wide(last, 0, 1, nc.vector.tensor_copy, psum_o)
-        out_wide(last, 1, 1, nc.scalar.copy, psum_p)
-        store(last, 1)
-        narrow_mm(last)
+        store_half(last, 1, 0)
+        out_wide(last, 1, 1, nc.scalar.copy, psum_c)
+        store_half(last, 1, 1)
+        narrow_mm(last, psum_r)
         narrow_out(last, nc.vector.tensor_copy)
         store(last, 2)

@@ -380,25 +380,8 @@ def tile_moralinear_pa_t_kernel(tc, x, weight, lora_a_weight, out):
             cols = slice(256 * q, 256 * q + 256)
             nc.vector.quantize_mx(out=w_codes[:, cols].bitcast(FP8X4), scales=w_scales[:, cols], in_=w_grp[q][:])
 
-        w_transpose(0, nc.vector.tensor_copy, psum_p, "p")
-        x_transpose(0)
-        x_out(0, nc.scalar.copy)
-        w_transpose(1, nc.scalar.copy, psum_p, "p")
-        w_quantise(0)
-        w_transpose(2, nc.vector.tensor_copy, psum_r, "r")
-        x_quantise(0)
-        w_quantise(1)
-        w_transpose(3, nc.scalar.copy, psum_r, "r")
-        w_quantise(2)
-        w_transpose(4, nc.scalar.copy, psum_c, "c")
-        x_transpose(1)
-        x_out(1, nc.scalar.copy)
-        plain_mm(0, 0)
-        plain_mm(0, 1)
-        w_quantise(3)
-        rotated_mm(0, 1, 0)
-        rotated_v(0, 1, 0)
-        w_quantise(4)
+        def a_quantise():
+            nc.vector.quantize_mx(out=a_codes[:].bitcast(FP8X4), scales=a_scales[:], in_=a_grp[:].rearrange("p q s -> p (q s)"))
 
         def a_prepare():
             for jj in range(2):
@@ -412,19 +395,58 @@ def tile_moralinear_pa_t_kernel(tc, x, weight, lora_a_weight, out):
                     in_=bank[:].rearrange("p j s q -> p j q s"),
                 )
 
-        for hb in range(N_HB - 1):
+        w_transpose(0, nc.vector.tensor_copy, psum_p, "p")
+        x_transpose(0)
+        x_out(0, nc.scalar.copy)
+        w_transpose(1, nc.scalar.copy, psum_p, "p")
+        w_quantise(0)
+        w_transpose(2, nc.scalar.copy, psum_r, "r")
+        x_quantise(0)
+        w_quantise(1)
+        w_transpose(3, nc.scalar.copy, psum_r, "r")
+        w_quantise(2)
+        w_transpose(4, nc.scalar.copy, psum_c, "c")
+        x_transpose(1)
+        x_out(1, nc.scalar.copy)
+        plain_mm(0, 0)
+        plain_mm(0, 1)
+        w_quantise(3)
+        rotated_mm(0, 1, 0)
+        rotated_v(0, 1, 0)
+
+        hb = 0
+        prev = -1
+        plain_out(hb, 0)
+        w_quantise(4)
+        plain_out(hb, 1)
+        x_quantise(hb + 1)
+        z_quantise(hb, 0)
+        rotated_mm(hb, 1, 1)
+        rotated_v(hb, 1, 1)
+        second_v(hb)
+        second_mm(hb)
+        a_prepare()
+        rotated_add(hb, 1, 0)
+        x_transpose(hb + 2)
+        x_out(hb + 2, nc.scalar.copy)
+        plain_mm(hb + 1, 0)
+        plain_mm(hb + 1, 1)
+        rotated_add(hb, 1, 1)
+        regroup(hb, 1)
+        second_w(hb)
+        rotated_mm(hb + 1, 1, 0)
+        rotated_v(hb + 1, 1, 0)
+        second_add(hb)
+        regroup(hb, 2)
+        a_quantise()
+        for hb in range(1, N_HB - 1):
             prev = hb - 1
             plain_out(hb, 0)
             plain_out(hb, 1)
-            second_v_part(hb, 1, 1, nc.vector)
-            second_v_part(hb, 0, 0, nc.scalar)
-            second_v_part(hb, 0, 1, nc.scalar)
-            second_v_part(hb, 1, 0, nc.scalar)
+            second_v(hb)
             rotated_mm(hb, 1, 1)
             rotated_v(hb, 1, 1)
             second_mm(hb)
-            if hb == 0:
-                a_prepare()
             rotated_add(hb, 1, 0)
             out_wide(prev, 0, 0, nc.scalar.copy, psum_o)
             out_wide(prev, 1, 0, nc.scalar.copy, psum_o)
@@ -450,8 +472,6 @@ def tile_moralinear_pa_t_kernel(tc, x, weight, lora_a_weight, out):
             store(prev, 2)
             second_add(hb)
             regroup(hb, 2)
-            if hb == 0:
-                nc.vector.quantize_mx(out=a_codes[:].bitcast(FP8X4), scales=a_scales[:], in_=a_grp[:].rearrange("p q s -> p (q s)"))
 
         last = N_HB - 1
         prev = last - 1

@@ -101,10 +101,10 @@ def tile_moralinear_pa_t_kernel(tc, x, weight, lora_a_weight, out):
         nc.vector.reciprocal(out=cot_t[:], in_=nsin_t[:])
         nc.vector.tensor_tensor(out=cot_t[:], in0=cot_t[:], in1=cos_t[:], op=ALU.mult)
 
-        w_codes = const.tile([P, OUT_DIM], U32, align_bytes=64)
-        w_scales = const.tile([P, OUT_DIM], U8, align_bytes=64)
-        a_codes = const.tile([P, R], U32, align_bytes=64)
-        a_scales = const.tile([P, R], U8, align_bytes=64)
+        w_codes = const.tile([P, OUT_DIM], U32, align_bytes=256)
+        w_scales = const.tile([P, OUT_DIM], U8, align_bytes=256)
+        a_codes = const.tile([P, R], U32, align_bytes=256)
+        a_scales = const.tile([P, R], U8, align_bytes=256)
         a_grp = const.tile([P, R, 4], BF16, align_bytes=64)
 
         state = {}
@@ -156,15 +156,15 @@ def tile_moralinear_pa_t_kernel(tc, x, weight, lora_a_weight, out):
         def x_quantise(hb):
             if not ok(hb):
                 return
-            xc = xq.tile([P, HB], U32, name="xc", tag="xc", align_bytes=64)
-            xs = xq.tile([P, HB], U8, name="xs", tag="xs", align_bytes=64)
+            xc = xq.tile([P, HB], U32, name="xc", tag="xc", align_bytes=256)
+            xs = xq.tile([P, HB], U8, name="xs", tag="xs", align_bytes=256)
             nc.vector.quantize_mx(out=xc[:].bitcast(FP8X4), scales=xs[:], in_=state[("xg", hb)][:])
             state[("x", hb)] = (xc, xs)
 
         def new_group(hb, n):
             state[("g", hb, n)] = gpool.tile([P, HB, 4], BF16, name="zg%d" % n, tag="zg%d" % n, align_bytes=64)
-            state[("zc", hb, n)] = zq.tile([P, HB], U32, name="zc%d" % n, tag="zc%d" % n, align_bytes=64)
-            state[("zs", hb, n)] = zq.tile([P, HB], U8, name="zs%d" % n, tag="zs%d" % n, align_bytes=64)
+            state[("zc", hb, n)] = zq.tile([P, HB], U32, name="zc%d" % n, tag="zc%d" % n, align_bytes=256)
+            state[("zs", hb, n)] = zq.tile([P, HB], U8, name="zs%d" % n, tag="zs%d" % n, align_bytes=256)
             if n > 0 and hb < N_HB - 1:
                 state[("zp", hb, n)] = ppool.tile([P, 4, HB], BF16, name="zp%d" % n, tag="zp%d" % n)
 
@@ -436,6 +436,10 @@ def tile_moralinear_pa_t_kernel(tc, x, weight, lora_a_weight, out):
         second_w(hb)
         rotated_mm(hb + 1, 1, 0)
         rotated_v(hb + 1, 1, 0)
+        x_transpose(hb + 3)
+        x_transpose(hb + 4)
+        x_out(hb + 3, nc.scalar.copy)
+        x_out(hb + 4, nc.scalar.copy)
         second_add(hb)
         regroup(hb, 2)
         a_quantise()
@@ -451,8 +455,8 @@ def tile_moralinear_pa_t_kernel(tc, x, weight, lora_a_weight, out):
             out_wide(prev, 0, 0, nc.scalar.copy, psum_o)
             out_wide(prev, 1, 0, nc.scalar.copy, psum_o)
             store(prev, 0)
-            x_transpose(hb + 2)
-            x_out(hb + 2, nc.scalar.copy)
+            x_transpose(hb + 4)
+            x_out(hb + 4, nc.scalar.copy)
             x_quantise(hb + 1)
             z_quantise(hb, 0)
             z_quantise(prev, 1)

@@ -33,8 +33,8 @@ def tile_moralinear_pa_t_kernel(tc, x, weight, lora_a_weight, out):
     nc = tc.nc
     x_blocks = x.flatten_outer_dims().rearrange("(b p i) k -> b p (i k)", p=P, i=4)
     out_blocks = out.flatten_outer_dims().rearrange("(b p i) c -> b p (i c)", p=P, i=4)
-    w_pairs = weight.rearrange("(q j p) k -> q p j k", j=2, p=P)
-    a_rows = lora_a_weight.rearrange("(j p) r -> p j r", p=P)
+    w_pairs = weight.rearrange("(q p j) k -> q p j k", j=2, p=P)
+    a_rows = lora_a_weight.rearrange("(p j) r -> p j r", j=4)
 
     with ExitStack() as ctx:
         const = ctx.enter_context(tc.tile_pool(name="const", bufs=1))
@@ -72,6 +72,8 @@ def tile_moralinear_pa_t_kernel(tc, x, weight, lora_a_weight, out):
             nc.sync.dma_start(out=xr[:], in_=x_blocks[b])
             x_raw.append(xr)
 
+        warm = const.tile([P, 512], BF16)
+        nc.gpsimd.memset(warm[:], 0.0)
         j_int = const.tile([P, 2], I32)
         nc.gpsimd.iota(j_int[:], pattern=[[P, 2]], base=0, channel_multiplier=1)
         ident_f = const.tile([P, P], F32)
@@ -373,7 +375,10 @@ def tile_moralinear_pa_t_kernel(tc, x, weight, lora_a_weight, out):
             bank = pool.tile([P, 2, 2, P], F32, name="wt", tag=tag)
             word_transposes(bank, w_raw[q][:].rearrange("p j k -> p (j k)").bitcast(F32), 0)
             wg = grp.tile([P, 4 * 256], BF16, name="wg", tag="wg", align_bytes=64)
-            words_out(copy, wg, bank)
+            copy(
+                out=wg[:].bitcast(F32).rearrange("p (t j u) -> p t j u", j=2, u=2),
+                in_=bank[:].rearrange("p j u t -> p t j u"),
+            )
             w_grp[q] = wg
 
         def w_quantise(q):
@@ -391,21 +396,33 @@ def tile_moralinear_pa_t_kernel(tc, x, weight, lora_a_weight, out):
                         r0 = P * SLOT_TO_CHUNK[s]
                         nc.tensor.transpose(bank[:, j, s, :], a_raw[:, 2 * jj + j, r0 : r0 + P], ident_b[:])
                 nc.scalar.copy(
-                    out=a_grp[:, 256 * jj : 256 * jj + 256, :].rearrange("p (j q) s -> p j q s", j=2),
-                    in_=bank[:].rearrange("p j s q -> p j q s"),
+                    out=a_grp[:].rearrange("p (q j) s -> p q j s", j=4)[:, :, 2 * jj : 2 * jj + 2, :],
+                    in_=bank[:].rearrange("p j s q -> p q j s"),
                 )
 
+        warm_bank = psum_o.tile([P, 512], F32, name="warm", tag="o")
+
+        def warm_up(count, width):
+            for turn in range(count):
+                nc.tensor.matmul(out=warm_bank[:, :width], lhsT=warm[:, :P], rhs=warm[:, :width], start=True, stop=True)
+
+        warm_up(6, 512)
         w_transpose(0, nc.vector.tensor_copy, psum_p, "p")
         x_transpose(0)
         x_out(0, nc.scalar.copy)
+        warm_up(1, 384)
         w_transpose(1, nc.scalar.copy, psum_p, "p")
+        warm_up(1, 384)
         w_quantise(0)
         w_transpose(2, nc.scalar.copy, psum_r, "r")
+        warm_up(1, 384)
         x_quantise(0)
         w_quantise(1)
         w_transpose(3, nc.scalar.copy, psum_r, "r")
+        warm_up(1, 384)
         w_quantise(2)
         w_transpose(4, nc.scalar.copy, psum_c, "c")
+        warm_up(1, 384)
         x_transpose(1)
         x_out(1, nc.scalar.copy)
         plain_mm(0, 0)

@@ -388,17 +388,16 @@ def tile_moralinear_pa_t_kernel(tc, x, weight, lora_a_weight, out):
         def a_quantise():
             nc.vector.quantize_mx(out=a_codes[:].bitcast(FP8X4), scales=a_scales[:], in_=a_grp[:].rearrange("p q s -> p (q s)"))
 
-        def a_prepare():
-            for jj in range(2):
-                bank = psum_o.tile([P, 2, 4, P], BF16, name="at", tag="o")
-                for j in range(2):
-                    for s in range(4):
-                        r0 = P * SLOT_TO_CHUNK[s]
-                        nc.tensor.transpose(bank[:, j, s, :], a_raw[:, 2 * jj + j, r0 : r0 + P], ident_b[:])
-                nc.scalar.copy(
-                    out=a_grp[:].rearrange("p (q j) s -> p q j s", j=4)[:, :, 2 * jj : 2 * jj + 2, :],
-                    in_=bank[:].rearrange("p j s q -> p q j s"),
-                )
+        def a_transpose(jj):
+            bank = psum_o.tile([P, 2, 4, P], BF16, name="at", tag="o")
+            for j in range(2):
+                for s in range(4):
+                    r0 = P * SLOT_TO_CHUNK[s]
+                    nc.tensor.transpose(bank[:, j, s, :], a_raw[:, 2 * jj + j, r0 : r0 + P], ident_b[:])
+            nc.scalar.copy(
+                out=a_grp[:].rearrange("p (q j) s -> p q j s", j=4)[:, :, 2 * jj : 2 * jj + 2, :],
+                in_=bank[:].rearrange("p j s q -> p q j s"),
+            )
 
         warm_bank = psum_o.tile([P, 512], F32, name="warm", tag="o")
 
@@ -410,19 +409,19 @@ def tile_moralinear_pa_t_kernel(tc, x, weight, lora_a_weight, out):
         w_transpose(0, nc.vector.tensor_copy, psum_p, "p")
         x_transpose(0)
         x_out(0, nc.scalar.copy)
-        warm_up(1, 384)
+        warm_up(1, 512)
         w_transpose(1, nc.scalar.copy, psum_p, "p")
-        warm_up(1, 384)
+        warm_up(1, 512)
         w_quantise(0)
         w_transpose(2, nc.scalar.copy, psum_r, "r")
-        warm_up(1, 384)
+        warm_up(1, 512)
         x_quantise(0)
         w_quantise(1)
         w_transpose(3, nc.scalar.copy, psum_r, "r")
-        warm_up(1, 384)
+        warm_up(1, 512)
         w_quantise(2)
         w_transpose(4, nc.scalar.copy, psum_c, "c")
-        warm_up(1, 384)
+        warm_up(1, 512)
         x_transpose(1)
         x_out(1, nc.scalar.copy)
         plain_mm(0, 0)
@@ -441,8 +440,9 @@ def tile_moralinear_pa_t_kernel(tc, x, weight, lora_a_weight, out):
         rotated_mm(hb, 1, 1)
         rotated_v(hb, 1, 1)
         second_v(hb)
+        a_transpose(0)
         second_mm(hb)
-        a_prepare()
+        a_transpose(1)
         rotated_add(hb, 1, 0)
         x_transpose(hb + 2)
         x_out(hb + 2, nc.scalar.copy)

import math
from contextlib import ExitStack

import concourse.bass as bass
import concourse.mybir as mybir
import concourse.tile as tile
from concourse.masks import make_identity

F32 = mybir.dt.float32
BF16 = mybir.dt.bfloat16
U32 = mybir.dt.uint32
U8 = mybir.dt.uint8
I32 = mybir.dt.int32
FP8X4 = mybir.dt.float8_e4m3fn_x4
ACT = mybir.ActivationFunctionType
ALU = mybir.AluOpType

P = 128
TOKENS = 4096
IN_DIM = 512
OUT_DIM = 1280
R = 512
HB = 256
N_HB = TOKENS // HB
W_TILES = OUT_DIM // P
SLOT_TO_CHUNK = (0, 2, 1, 3)
PIN = True

FLOPS = 2 * TOKENS * IN_DIM * OUT_DIM + 2 * TOKENS * R * 3 * R


def tile_moralinear_pa_t_kernel(tc, x, weight, lora_a_weight, out):
    nc = tc.nc
    x_blocks = x.flatten_outer_dims().rearrange("(b p i) k -> b p (i k)", p=P, i=4)
    out_blocks = out.flatten_outer_dims().rearrange("(b p i) c -> b p (i c)", p=P, i=4)
    w_pairs = weight.rearrange("(q p j) k -> q p j k", j=2, p=P)
    a_rows = lora_a_weight.rearrange("(p j) r -> p j r", j=4)

    with ExitStack() as ctx:
        const = ctx.enter_context(tc.tile_pool(name="const", bufs=1))
        xin = ctx.enter_context(tc.tile_pool(name="xin", bufs=8))
        win = ctx.enter_context(tc.tile_pool(name="win", bufs=5))
        grp = ctx.enter_context(tc.tile_pool(name="grp", bufs=5))
        xq = ctx.enter_context(tc.tile_pool(name="xq", bufs=6))
        vpool = ctx.enter_context(tc.tile_pool(name="vpool", bufs=4))
        gpool = ctx.enter_context(tc.tile_pool(name="gpool", bufs=3))
        ppool = ctx.enter_context(tc.tile_pool(name="ppool", bufs=3))
        zq = ctx.enter_context(tc.tile_pool(name="zq", bufs=3))
        opool = ctx.enter_context(tc.tile_pool(name="opool", bufs=3))
        psum_p = ctx.enter_context(tc.psum_pool(name="psum_p", bufs=2))
        psum_r = ctx.enter_context(tc.psum_pool(name="psum_r", bufs=2))
        psum_c = ctx.enter_context(tc.psum_pool(name="psum_c", bufs=1))
        psum_o = ctx.enter_context(tc.psum_pool(name="psum_o", bufs=3))
        if PIN:
            ctx.enter_context(tc.manual_schedule())

        x_raw = []
        w_raw = []
        xr0 = xin.tile([P, 4 * IN_DIM], BF16, name="x_raw", tag="x_raw")
        x_raw.append(xr0)
        for q in range(W_TILES // 2):
            wr = win.tile([P, 2, IN_DIM], BF16, name="w_raw", tag="w_raw")
            nc.sync.dma_start(out=wr[:], in_=w_pairs[q])
            w_raw.append(wr)
            if q == 0:
                nc.sync.dma_start(out=xr0[:, : 2 * IN_DIM], in_=x_blocks[0][:, : 2 * IN_DIM])
        nc.sync.dma_start(out=xr0[:, 2 * IN_DIM :], in_=x_blocks[0][:, 2 * IN_DIM :])
        a_raw = const.tile([P, 4, R], BF16)
        nc.sync.dma_start(out=a_raw[:], in_=a_rows)
        for b in range(1, TOKENS // 512):
            xr = xin.tile([P, 4 * IN_DIM], BF16, name="x_raw", tag="x_raw")
            nc.sync.dma_start(out=xr[:], in_=x_blocks[b])
            x_raw.append(xr)

        warm = const.tile([P, 512], BF16)
        nc.gpsimd.memset(warm[:], 0.0)
        j_int = const.tile([P, 2], I32)
        nc.gpsimd.iota(j_int[:], pattern=[[P, 2]], base=0, channel_multiplier=1)
        ident_f = const.tile([P, P], F32)
        make_identity(nc, ident_f[:])
        ident_b = const.tile([P, P], BF16)
        make_identity(nc, ident_b[:])

        j_f = const.tile([P, 2], F32)
        nc.vector.tensor_copy(out=j_f[:], in_=j_int[:])
        theta = const.tile([P, 2], F32)
        nc.scalar.activation(out=theta[:], in_=j_f[:], func=ACT.Exp, scale=-math.log(10000.0) / 256.0)
        ang = const.tile([P, 4], F32)
        nc.vector.tensor_copy(out=ang[:, 0:2], in_=theta[:])
        nc.vector.tensor_scalar(out=ang[:, 2:4], in0=theta[:], scalar1=2.0, scalar2=None, op0=ALU.mult)
        sin_t = const.tile([P, 4], F32)
        nc.scalar.activation(out=sin_t[:], in_=ang[:], func=ACT.Sin)
        half_t = const.tile([P, 4], F32)
        nc.scalar.activation(out=half_t[:], in_=ang[:], func=ACT.Sin, scale=0.5)
        nsin_t = const.tile([P, 4], F32)
        nc.vector.tensor_scalar(out=nsin_t[:], in0=sin_t[:], scalar1=-1.0, scalar2=None, op0=ALU.mult)
        sq_t = const.tile([P, 4], F32)
        nc.vector.tensor_tensor(out=sq_t[:], in0=half_t[:], in1=half_t[:], op=ALU.mult)
        cos_t = const.tile([P, 4], F32)
        nc.vector.tensor_scalar(out=cos_t[:], in0=sq_t[:], scalar1=-2.0, scalar2=1.0, op0=ALU.mult, op1=ALU.add)

        cot_t = const.tile([P, 4], F32)
        nc.vector.reciprocal(out=cot_t[:], in_=nsin_t[:])
        nc.vector.tensor_tensor(out=cot_t[:], in0=cot_t[:], in1=cos_t[:], op=ALU.mult)

        w_codes = const.tile([P, OUT_DIM], U32, align_bytes=256)
        w_scales = const.tile([P, OUT_DIM], U8, align_bytes=256)
        a_codes = const.tile([P, R], U32, align_bytes=256)
        a_scales = const.tile([P, R], U8, align_bytes=256)
        a_grp = const.tile([P, R, 4], BF16, align_bytes=64)

        state = {}
        tags = ((psum_p, "p"), (psum_r, "r"), (psum_c, "c"), (psum_o, "o"))

        def tag_of(pool):
            return [tag for known, tag in tags if known is pool][0]

        def ok(hb):
            return 0 <= hb < N_HB

        def mx(out_ap, l_codes, l_scales, r_codes, r_scales, start, stop):
            nc.tensor.matmul_mx(
                out=out_ap,
                lhsT=l_codes.bitcast(FP8X4),
                lhsT_scale=l_scales,
                rhs=r_codes.bitcast(FP8X4),
                rhs_scale=r_scales,
                start=start,
                stop=stop,
            )

        def word_transposes(bank, raw_words, first):
            for i in range(2):
                for u in range(2):
                    c0 = first + 256 * i + 128 * u
                    nc.tensor.transpose(bank[:, i, u, :], raw_words[:, c0 : c0 + P], ident_f[:])

        def words_out(engine_copy, dst, bank):
            engine_copy(
                out=dst[:].bitcast(F32).rearrange("p (i t u) -> p i t u", i=2, u=2),
                in_=bank[:].rearrange("p i u t -> p i t u"),
            )

        def x_transpose(hb):
            if not ok(hb):
                return
            bank = psum_o.tile([P, 2, 2, P], F32, name="xt", tag="o")
            word_transposes(bank, x_raw[hb // 2][:].bitcast(F32), 512 * (hb % 2))
            state[("xt", hb)] = bank

        def x_out(hb, copy):
            if not ok(hb):
                return
            xg = grp.tile([P, 4 * HB], BF16, name="xg", tag="xg", align_bytes=64)
            words_out(copy, xg, state[("xt", hb)])
            state[("xg", hb)] = xg

        def x_quantise(hb):
            if not ok(hb):
                return
            xc = xq.tile([P, HB], U32, name="xc", tag="xc", align_bytes=256)
            xs = xq.tile([P, HB], U8, name="xs", tag="xs", align_bytes=256)
            nc.vector.quantize_mx(out=xc[:].bitcast(FP8X4), scales=xs[:], in_=state[("xg", hb)][:])
            state[("x", hb)] = (xc, xs)

        def new_group(hb, n):
            state[("g", hb, n)] = gpool.tile([P, HB, 4], BF16, name="zg%d" % n, tag="zg%d" % n, align_bytes=64)
            state[("zc", hb, n)] = zq.tile([P, HB], U32, name="zc%d" % n, tag="zc%d" % n, align_bytes=256)
            state[("zs", hb, n)] = zq.tile([P, HB], U8, name="zs%d" % n, tag="zs%d" % n, align_bytes=256)
            if n > 0 and hb < N_HB - 1:
                state[("zp", hb, n)] = ppool.tile([P, 4, HB], BF16, name="zp%d" % n, tag="zp%d" % n)

        def plain_mm(hb, i):
            if not ok(hb):
                return
            if i == 0:
                new_group(hb, 0)
            xc, xs = state[("x", hb)]
            bank = psum_p.tile([P, 4, P], F32, name="g0", tag="p")
            t = slice(P * i, P * i + P)
            for s in range(4):
                w = slice(P * SLOT_TO_CHUNK[s], P * SLOT_TO_CHUNK[s] + P)
                mx(bank[:, s, :], w_codes[:, w], w_scales[:, w], xc[:, t], xs[:, t], True, True)
            state[("g0", hb, i)] = bank

        def plain_out(hb, i):
            if not ok(hb):
                return
            t = slice(P * i, P * i + P)
            nc.vector.tensor_copy(out=state[("g", hb, 0)][:, t, :], in_=state[("g0", hb, i)][:].rearrange("p s t -> p t s"))

        def rotated_mm(hb, n, tm, pool=psum_r, tag="r"):
            if not ok(hb):
                return
            if tm == 0:
                new_group(hb, n)
            xc, xs = state[("x", hb)]
            bank = pool.tile([P, 2, HB], F32, name="z", tag=tag)
            state[("z", hb, n, tm)] = bank
            for ab in range(2):
                jw = (4 * n + tm + 2 * ab) % W_TILES
                w = slice(P * jw, P * jw + P)
                mx(bank[:, ab, :], w_codes[:, w], w_scales[:, w], xc[:], xs[:], True, True)

        def rotated_v(hb, n, tm):
            if not ok(hb):
                return
            bank = state[("z", hb, n, tm)]
            k = 2 * (n - 1) + tm
            v = vpool.tile([P, 2, HB], F32, name="v", tag="v")
            nc.scalar.activation(out=v[:, 0, :], in_=bank[:, 1, :], func=ACT.Copy, scale=nsin_t[:, k : k + 1])
            nc.scalar.activation(out=v[:, 1, :], in_=bank[:, 0, :], func=ACT.Copy, scale=sin_t[:, k : k + 1])
            state[("v", hb, n, tm)] = v

        def rotated_add(hb, n, tm):
            if not ok(hb):
                return
            bank, v = state[("z", hb, n, tm)], state[("v", hb, n, tm)]
            k = 2 * (n - 1) + tm
            if hb == N_HB - 1:
                nc.vector.scalar_tensor_tensor(
                    out=state[("g", hb, n)][:, :, 2 * tm : 2 * tm + 2],
                    in0=bank[:].rearrange("p a t -> p t a"),
                    scalar=cos_t[:, k : k + 1],
                    in1=v[:].rearrange("p a t -> p t a"),
                    op0=ALU.mult,
                    op1=ALU.add,
                )
            else:
                nc.vector.scalar_tensor_tensor(
                    out=state[("zp", hb, n)][:, 2 * tm : 2 * tm + 2, :],
                    in0=bank[:],
                    scalar=cos_t[:, k : k + 1],
                    in1=v[:],
                    op0=ALU.mult,
                    op1=ALU.add,
                )

        def second_mm(hb):
            if not ok(hb) or hb == N_HB - 1:
                return
            xc, xs = state[("x", hb)]
            new_group(hb, 2)
            bank = psum_c.tile([P, 2, HB], F32, name="zc", tag="c")
            for tm in range(2):
                w = slice(P * (8 + tm), P * (8 + tm) + P)
                mx(bank[:, tm, :], w_codes[:, w], w_scales[:, w], xc[:], xs[:], True, True)
            state[("c", hb)] = bank

        def second_v_part(hb, i, tm, engine):
            if not ok(hb) or hb == N_HB - 1:
                return
            if ("v2", hb) not in state:
                state[("v2", hb)] = vpool.tile([P, 2, HB], F32, name="v2", tag="v2")
            out = state[("v2", hb)][:, tm, P * i : P * i + P]
            src = state[("g0", hb, i)][:, 2 * tm, :]
            scale = nsin_t[:, 2 + tm : 3 + tm]
            if engine is nc.scalar:
                nc.scalar.activation(out=out, in_=src, func=ACT.Copy, scale=scale)
            else:
                nc.vector.tensor_scalar(out=out, in0=src, scalar1=scale, scalar2=None, op0=ALU.mult)

        def second_v(hb):
            for i in range(2):
                for tm in range(2):
                    second_v_part(hb, i, tm, nc.scalar)

        def second_w(hb, engine=nc.vector):
            if not ok(hb) or hb == N_HB - 1:
                return
            v = state[("v2", hb)]
            w2 = vpool.tile([P, 2, HB], F32, name="w2", tag="w2")
            for tm in range(2):
                engine.tensor_scalar(
                    out=w2[:, tm, :],
                    in0=v[:, tm, :],
                    scalar1=cot_t[:, 2 + tm : 3 + tm],
                    scalar2=0.0,
                    op0=ALU.mult,
                    op1=ALU.add,
                )
            state[("w2", hb)] = w2

        def second_add(hb):
            if not ok(hb) or hb == N_HB - 1:
                return
            bank = state[("c", hb)]
            zp = state[("zp", hb, 2)]
            for half, (scale, other) in enumerate(((cos_t, "v2"), (sin_t, "w2"))):
                for tm in range(2):
                    nc.vector.scalar_tensor_tensor(
                        out=zp[:, 2 * tm + half, :],
                        in0=bank[:, tm, :],
                        scalar=scale[:, 2 + tm : 3 + tm],
                        in1=state[(other, hb)][:, tm, :],
                        op0=ALU.mult,
                        op1=ALU.add,
                    )

        def regroup(hb, n):
            if not ok(hb) or hb == N_HB - 1:
                return
            nc.gpsimd.tensor_scalar(
                out=state[("g", hb, n)][:],
                in0=state[("zp", hb, n)][:].rearrange("p s t -> p t s"),
                scalar1=1.0,
                scalar2=0.0,
                op0=ALU.mult,
                op1=ALU.add,
            )

        def z_quantise(hb, n):
            if not ok(hb):
                return
            nc.vector.quantize_mx(
                out=state[("zc", hb, n)][:].bitcast(FP8X4),
                scales=state[("zs", hb, n)][:],
                in_=state[("g", hb, n)][:].rearrange("p t s -> p (t s)"),
            )

        def out_wide(hb, i, c, copy, pool):
            if not ok(hb):
                return
            if i == 0:
                state[("o", hb, c)] = opool.tile([P, 2, 512], F32, name="o_sb%d" % c, tag="o_sb%d" % c)
            xc, xs = state[("x", hb)]
            zc = state[("zc", hb, c)]
            zs = state[("zs", hb, c)]
            t = slice(P * i, P * i + P)
            cols = slice(512 * c, 512 * c + 512)
            bank = pool.tile([P, 512], F32, name="o", tag=tag_of(pool))
            mx(bank[:], xc[:, t], xs[:, t], w_codes[:, cols], w_scales[:, cols], True, False)
            mx(bank[:], zc[:, t], zs[:, t], a_codes[:], a_scales[:], False, True)
            copy(out=state[("o", hb, c)][:, i, :], in_=bank[:])

        def narrow_mm(hb, pool=psum_o):
            if not ok(hb):
                return
            state[("o", hb, 2)] = opool.tile([P, 2, 256], F32, name="o_sb2", tag="o_sb2")
            xc, xs = state[("x", hb)]
            zc = state[("zc", hb, 2)]
            zs = state[("zs", hb, 2)]
            bank = pool.tile([P, 2, 256], F32, name="o2", tag=tag_of(pool))
            for i in range(2):
                t = slice(P * i, P * i + P)
                mx(bank[:, i, :], xc[:, t], xs[:, t], w_codes[:, 1024:1280], w_scales[:, 1024:1280], True, False)
                mx(bank[:, i, :], zc[:, t], zs[:, t], a_codes[:, 0:256], a_scales[:, 0:256], False, True)
            state[("n", hb)] = bank

        def narrow_out(hb, copy):
            if not ok(hb):
                return
            copy(out=state[("o", hb, 2)][:], in_=state[("n", hb)][:])

        def narrow_half(hb, i, copy):
            copy(out=state[("o", hb, 2)][:, i, :], in_=state[("n", hb)][:, i, :])

        def store_half(hb, c, i):
            dst = out_blocks[hb // 2].rearrange("p (i c) -> p i c", i=4)
            nc.sync.dma_start(
                out=dst[:, 2 * (hb % 2) + i, 512 * c : min(512 * c + 512, OUT_DIM)],
                in_=state[("o", hb, c)][:, i, :],
            )

        def store(hb, c):
            if not ok(hb):
                return
            dst = out_blocks[hb // 2].rearrange("p (i c) -> p i c", i=4)
            h = hb % 2
            nc.sync.dma_start(out=dst[:, 2 * h : 2 * h + 2, 512 * c : min(512 * c + 512, OUT_DIM)], in_=state[("o", hb, c)][:])

        w_grp = {}

        def w_transpose(q, copy, pool, tag):
            bank = pool.tile([P, 2, 2, P], F32, name="wt", tag=tag)
            word_transposes(bank, w_raw[q][:].rearrange("p j k -> p (j k)").bitcast(F32), 0)
            wg = grp.tile([P, 4 * 256], BF16, name="wg", tag="wg", align_bytes=64)
            copy(
                out=wg[:].bitcast(F32).rearrange("p (t j u) -> p t j u", j=2, u=2),
                in_=bank[:].rearrange("p j u t -> p t j u"),
            )
            w_grp[q] = wg

        def w_quantise(q):
            cols = slice(256 * q, 256 * q + 256)
            nc.vector.quantize_mx(out=w_codes[:, cols].bitcast(FP8X4), scales=w_scales[:, cols], in_=w_grp[q][:])

        def a_quantise():
            nc.vector.quantize_mx(out=a_codes[:].bitcast(FP8X4), scales=a_scales[:], in_=a_grp[:].rearrange("p q s -> p (q s)"))

        def a_transpose(jj):
            bank = psum_o.tile([P, 2, 4, P], BF16, name="at", tag="o")
            for j in range(2):
                for s in range(4):
                    r0 = P * SLOT_TO_CHUNK[s]
                    nc.tensor.transpose(bank[:, j, s, :], a_raw[:, 2 * jj + j, r0 : r0 + P], ident_b[:])
            nc.scalar.copy(
                out=a_grp[:].rearrange("p (q j) s -> p q j s", j=4)[:, :, 2 * jj : 2 * jj + 2, :],
                in_=bank[:].rearrange("p j s q -> p q j s"),
            )

        warm_bank = psum_o.tile([P, 512], F32, name="warm", tag="o")

        def warm_up(count, width):
            for turn in range(count):
                nc.tensor.matmul(out=warm_bank[:, :width], lhsT=warm[:, :P], rhs=warm[:, :width], start=True, stop=True)

        warm_up(6, 512)
        w_transpose(0, nc.vector.tensor_copy, psum_p, "p")
        x_transpose(0)
        x_out(0, nc.scalar.copy)
        warm_up(1, 512)
        w_transpose(1, nc.scalar.copy, psum_p, "p")
        warm_up(1, 512)
        w_quantise(0)
        w_transpose(2, nc.scalar.copy, psum_r, "r")
        warm_up(1, 512)
        x_quantise(0)
        w_quantise(1)
        w_transpose(3, nc.scalar.copy, psum_r, "r")
        warm_up(1, 512)
        w_quantise(2)
        w_transpose(4, nc.scalar.copy, psum_c, "c")
        warm_up(1, 512)
        x_transpose(1)
        x_out(1, nc.scalar.copy)
        plain_mm(0, 0)
        plain_mm(0, 1)
        w_quantise(3)
        rotated_mm(0, 1, 0)
        rotated_v(0, 1, 0)

        hb = 0
        prev = -1
        plain_out(hb, 0)
        w_quantise(4)
        plain_out(hb, 1)
        x_quantise(hb + 1)
        z_quantise(hb, 0)
        rotated_mm(hb, 1, 1)
        rotated_v(hb, 1, 1)
        second_v(hb)
        a_transpose(0)
        second_mm(hb)
        a_transpose(1)
        rotated_add(hb, 1, 0)
        x_transpose(hb + 2)
        x_out(hb + 2, nc.scalar.copy)
        plain_mm(hb + 1, 0)
        plain_mm(hb + 1, 1)
        rotated_add(hb, 1, 1)
        regroup(hb, 1)
        second_w(hb)
        rotated_mm(hb + 1, 1, 0)
        rotated_v(hb + 1, 1, 0)
        x_transpose(hb + 3)
        x_transpose(hb + 4)
        x_out(hb + 3, nc.scalar.copy)
        x_out(hb + 4, nc.scalar.copy)
        second_add(hb)
        regroup(hb, 2)
        a_quantise()
        for hb in range(1, N_HB - 1):
            prev = hb - 1
            plain_out(hb, 0)
            plain_out(hb, 1)
            second_v(hb)
            rotated_mm(hb, 1, 1)
            rotated_v(hb, 1, 1)
            second_mm(hb)
            rotated_add(hb, 1, 0)
            out_wide(prev, 0, 0, nc.scalar.copy, psum_o)
            out_wide(prev, 1, 0, nc.scalar.copy, psum_o)
            store(prev, 0)
            x_transpose(hb + 4)
            x_out(hb + 4, nc.scalar.copy)
            x_quantise(hb + 1)
            z_quantise(hb, 0)
            z_quantise(prev, 1)
            z_quantise(prev, 2)
            plain_mm(hb + 1, 0)
            plain_mm(hb + 1, 1)
            rotated_add(hb, 1, 1)
            regroup(hb, 1)
            second_w(hb)
            rotated_mm(hb + 1, 1, 0)
            rotated_v(hb + 1, 1, 0)
            out_wide(prev, 0, 1, nc.scalar.copy, psum_o)
            out_wide(prev, 1, 1, nc.scalar.copy, psum_o)
            store(prev, 1)
            narrow_mm(prev)
            narrow_out(prev, nc.scalar.copy)
            store(prev, 2)
            second_add(hb)
            regroup(hb, 2)

        last = N_HB - 1
        prev = last - 1
        rotated_mm(last, 2, 0, psum_c, "c")
        rotated_mm(last, 1, 1)
        plain_out(last, 0)
        plain_out(last, 1)
        rotated_v(last, 1, 1)
        rotated_v(last, 2, 0)
        out_wide(prev, 0, 0, nc.scalar.copy, psum_o)
        store_half(prev, 0, 0)
        rotated_mm(last, 2, 1, psum_p, "p")
        rotated_add(last, 1, 0)
        z_quantise(last, 0)
        z_quantise(prev, 1)
        z_quantise(prev, 2)
        out_wide(prev, 1, 0, nc.scalar.copy, psum_o)
        store_half(prev, 0, 1)
        rotated_v(last, 2, 1)
        rotated_add(last, 1, 1)
        out_wide(prev, 0, 1, nc.scalar.copy, psum_o)
        store_half(prev, 1, 0)
        out_wide(prev, 1, 1, nc.scalar.copy, psum_p)
        store_half(prev, 1, 1)
        rotated_add(last, 2, 0)
        z_quantise(last, 1)
        narrow_mm(prev, psum_r)
        narrow_out(prev, nc.scalar.copy)
        store(prev, 2)
        rotated_add(last, 2, 1)
        out_wide(last, 0, 0, nc.scalar.copy, psum_o)
        store_half(last, 0, 0)
        out_wide(last, 1, 0, nc.scalar.copy, psum_o)
        store_half(last, 0, 1)
        z_quantise(last, 2)
        out_wide(last, 0, 1, nc.vector.tensor_copy, psum_o)
        store_half(last, 1, 0)
        out_wide(last, 1, 1, nc.scalar.copy, psum_c)
        store_half(last, 1, 1)
        narrow_mm(last, psum_r)
        narrow_out(last, nc.vector.tensor_copy)
        store(last, 2)
